import numpy as np
import ml_dtypes


def mxq(x, axis, fmt="e4m3"):
    dtype, down = {"e4m3": (ml_dtypes.float8_e4m3fn, 7), "e5m2": (ml_dtypes.float8_e5m2, 14)}[fmt]
    v = np.moveaxis(np.asarray(x, np.float32).astype(ml_dtypes.bfloat16).astype(np.float64), axis, -1)
    blocks = v.reshape(v.shape[:-1] + (-1, 32))
    amax = np.abs(blocks).max(-1, keepdims=True)
    byte = np.maximum(np.where(amax > 0, np.frexp(amax)[1] - 1 + 127, 0) - down, 1)
    scale = np.exp2(byte - 127.0)
    codes = (blocks / scale).astype(np.float32).astype(dtype).astype(np.float64)
    return np.moveaxis((codes * scale).reshape(v.shape), -1, axis)


WIDE = False


def mx_kscale(k):
    if not WIDE:
        return np.ones(k)
    levels = np.array([10, -10, 5, -5, 0])
    a = np.random.permutation(np.resize(levels, k // 512 * 4)).reshape(k // 512, 4)
    idx = np.arange(k)
    return np.exp2(a[idx // 512, idx % 128 // 32])


BF16 = ml_dtypes.bfloat16


def bf(x):
    return np.asarray(x, np.float32).astype(BF16)


def f64(x):
    return np.asarray(x).astype(np.float64)


B, P_DIM, H_DIM, X_DIM = 512, 512, 1024, 512


def sigmoid(v):
    return 1.0 / (1.0 + np.exp(-v))


def setup_inputs():
    sp, sh, sx = mx_kscale(P_DIM), mx_kscale(H_DIM), mx_kscale(X_DIM)

    def lin_w(in_d, s):
        return bf(np.random.standard_normal((H_DIM, in_d)) * 0.6 / np.sqrt(in_d) / s[None, :])

    def lin_b():
        return bf(np.random.standard_normal(H_DIM) * 0.5)

    return {
        "P": bf(np.random.standard_normal((B, P_DIM)) * sp),
        "hidden": bf(np.random.standard_normal((B, H_DIM)) * sh),
        "cell": bf(np.random.standard_normal((B, H_DIM))),
        "ext_input": bf(np.random.standard_normal((B, X_DIM)) * sx),
        "W_pi": lin_w(P_DIM, sp), "b_pi": lin_b(),
        "W_pf": lin_w(P_DIM, sp), "b_pf": lin_b(),
        "W_pg": lin_w(P_DIM, sp), "b_pg": lin_b(),
        "W_po": lin_w(P_DIM, sp), "b_po": lin_b(),
        "W_hi": lin_w(H_DIM, sh), "W_hf": lin_w(H_DIM, sh),
        "W_hg": lin_w(H_DIM, sh), "W_ho": lin_w(H_DIM, sh),
        "W_xi": lin_w(X_DIM, sx), "W_xf": lin_w(X_DIM, sx),
        "W_xg": lin_w(X_DIM, sx), "W_xo": lin_w(X_DIM, sx),
    }


def reference(P, hidden, cell, ext_input,
              W_pi, b_pi, W_pf, b_pf, W_pg, b_pg, W_po, b_po,
              W_hi, W_hf, W_hg, W_ho,
              W_xi, W_xf, W_xg, W_xo):
    Wp = np.concatenate([f64(W_pi), f64(W_pf), f64(W_pg), f64(W_po)], axis=0)
    bp = np.concatenate([f64(b_pi), f64(b_pf), f64(b_pg), f64(b_po)], axis=0)
    Wh = np.concatenate([f64(W_hi), f64(W_hf), f64(W_hg), f64(W_ho)], axis=0)
    Wx = np.concatenate([f64(W_xi), f64(W_xf), f64(W_xg), f64(W_xo)], axis=0)
    gates = ((mxq(f64(P), 1, "e4m3") @ mxq(Wp, 1, "e4m3").T) + bp
             + (mxq(f64(hidden), 1, "e4m3") @ mxq(Wh, 1, "e4m3").T)
             + (mxq(f64(ext_input), 1, "e4m3") @ mxq(Wx, 1, "e4m3").T))
    gi, gf, gg, go = np.split(gates, 4, axis=-1)
    i = sigmoid(gi)
    f = sigmoid(gf)
    g = np.tanh(gg)
    o = sigmoid(go)
    c_new = f * f64(cell) + i * g
    h_new = o * np.tanh(c_new)
    return (h_new, c_new)

@@ -1,0 +1,308 @@
+from contextlib import ExitStack
+
+import concourse.mybir as mybir
+from concourse.masks import make_identity
+
+F32 = mybir.dt.float32
+BF16 = mybir.dt.bfloat16
+U32 = mybir.dt.uint32
+U8 = mybir.dt.uint8
+FP8X4 = mybir.dt.float8_e4m3fn_x4
+ACT = mybir.ActivationFunctionType
+ALU = mybir.AluOpType
+
+FLOPS = 2 * 512 * 2048 * 4096
+
+NB_RAW = 5
+N_BLOCKS = 8
+
+
+def tile_structuredlstmcell_kernel(
+    tc, P, hidden, cell, ext_input,
+    W_pi, b_pi, W_pf, b_pf, W_pg, b_pg, W_po, b_po,
+    W_hi, W_hf, W_hg, W_ho,
+    W_xi, W_xf, W_xg, W_xo,
+    out_0, out_1,
+):
+    nc = tc.nc
+    w_src = [
+        [W_pi, W_pf, W_po, W_pg],
+        [W_xi, W_xf, W_xo, W_xg],
+        [W_hi, W_hf, W_ho, W_hg],
+    ]
+    k_src = [512, 512, 1024]
+    biases = [b_pi, b_pf, b_po, b_pg]
+    acts = [P, ext_input, hidden]
+
+    with ExitStack() as ctx:
+        ctx.enter_context(tc.manual_schedule())
+        const = ctx.enter_context(tc.tile_pool(name="const", bufs=1))
+        rawp = ctx.enter_context(tc.tile_pool(name="rawp", bufs=NB_RAW))
+        gpool = ctx.enter_context(tc.tile_pool(name="gpool", bufs=4))
+        cpool = ctx.enter_context(tc.tile_pool(name="cpool", bufs=6))
+        prep = ctx.enter_context(tc.tile_pool(name="prep", bufs=3))
+        outp = ctx.enter_context(tc.tile_pool(name="outp", bufs=3))
+        psum = ctx.enter_context(tc.psum_pool(name="psum", bufs=1))
+
+        ident_f = const.tile([128, 128], F32, name="ident_f")
+        make_identity(nc, ident_f[:])
+        bz = const.tile([128, 512], BF16, name="bz")
+        nc.vector.memset(bz[:], 0.0)
+        warm = const.tile([128, 1], F32, name="warm")
+        nc.vector.memset(warm[:], 0.0)
+        for gi in range(4):
+            nc.scalar.dma_start(
+                out=bz[2 * gi:2 * gi + 2, :],
+                in_=biases[gi].rearrange("(r n) -> r n", r=2),
+            )
+        nc.scalar.activation(out=warm[:], in_=warm[:], func=ACT.Sigmoid)
+        ident_b = const.tile([128, 128], BF16, name="ident_b")
+        nc.vector.tensor_copy(out=ident_b[:], in_=ident_f[:])
+        bias_sb = const.tile([128, 4, 1024], F32, name="bias_sb")
+
+        raw_act = []
+        for s in range(3):
+            raw_act.append(const.tile([128, 4 * k_src[s]], BF16, name="ra%d" % s))
+        cell_sb = const.tile([128, 4, 1024], BF16, name="cell_sb")
+        acodes = const.tile([128, 4, 512], U32, name="acodes", align_bytes=64)
+        ascales = const.tile([128, 4, 512], U8, name="ascales", align_bytes=64)
+
+        def load_act(s):
+            nc.sync.dma_start(
+                out=raw_act[s][:],
+                in_=acts[s].rearrange("(p t) k -> p (t k)", t=4),
+            )
+
+        raw_w = {}
+
+        def load_w(j, s):
+            k = k_src[s]
+            t = rawp.tile([128, 4 * k], BF16, name="rw%d" % s, tag="rw%d" % s)
+            for gi in range(4):
+                nc.sync.dma_start(
+                    out=t[:, gi * k:(gi + 1) * k],
+                    in_=w_src[s][gi][j * 128:(j + 1) * 128, :],
+                )
+            raw_w[(j, s)] = t
+
+        load_act(0)
+        load_act(1)
+        load_w(0, 0)
+        load_w(0, 1)
+        load_act(2)
+        load_w(0, 2)
+        load_w(1, 0)
+        load_w(1, 1)
+        load_w(1, 2)
+        nc.sync.dma_start(
+            out=cell_sb[:].rearrange("p t h -> p (t h)"),
+            in_=cell.rearrange("(p t) h -> p (t h)", t=4),
+        )
+        for j in range(2, NB_RAW):
+            for s in range(3):
+                load_w(j, s)
+
+        def chunks_of(tiles, half):
+            if half == 0:
+                return [(tiles[0], 256, 0), (tiles[1], 256, 0)]
+            return [(tiles[2], 512, 0), (tiles[2], 512, 256)]
+
+        def transposes(chunks):
+            banks = []
+            for ci in range(2):
+                raw, kw, off = chunks[ci]
+                rw = raw[:].bitcast(F32)
+                for a in range(2):
+                    slot = 2 * ci + a
+                    xt = psum.tile([128, 2, 256], F32, name="xt%d" % slot, tag="xt%d" % slot)
+                    for g2 in range(2):
+                        for u in range(2):
+                            col = (2 * a + g2) * kw + off + 128 * u
+                            nc.tensor.transpose(
+                                xt[:, u, g2 * 128:(g2 + 1) * 128],
+                                rw[:, col:col + 128],
+                                ident_f[:],
+                            )
+                    banks.append(xt)
+            return banks
+
+        def evacuate(banks, engines):
+            grps = []
+            for ci in range(2):
+                grp = gpool.tile([128, 2048], BF16, name="grp", tag="grp", align_bytes=64)
+                gw = grp[:].bitcast(F32)
+                for a in range(2):
+                    slot = 2 * ci + a
+                    dst = gw[:, a * 512:(a + 1) * 512].rearrange("p (n u) -> p n u", u=2)
+                    src = banks[slot][:].rearrange("p u n -> p n u")
+                    if engines[slot] == "s":
+                        nc.scalar.copy(out=dst, in_=src)
+                    else:
+                        nc.vector.tensor_copy(out=dst, in_=src)
+                grps.append(grp)
+            return grps
+
+        def quantise_act(grps, half):
+            for ci in range(2):
+                c = 2 * half + ci
+                nc.vector.quantize_mx(
+                    out=acodes[:, c, :].bitcast(FP8X4),
+                    scales=ascales[:, c, :],
+                    in_=grps[ci][:],
+                )
+
+        def quantise_w(grps):
+            res = []
+            for ci in range(2):
+                wc = cpool.tile([128, 512], U32, name="wc", tag="wc", align_bytes=64)
+                ws = cpool.tile([128, 512], U8, name="ws", tag="ws", align_bytes=64)
+                nc.vector.quantize_mx(out=wc[:].bitcast(FP8X4), scales=ws[:], in_=grps[ci][:])
+                res.append((wc, ws))
+            return res
+
+        acc = [None, None, None, None]
+
+        def new_acc(bt):
+            acc[bt] = psum.tile([128, 512], F32, name="acc%d" % bt, tag="acc%d" % bt)
+
+        def mx_passes(half, q):
+            for bt in range(4):
+                if half == 0:
+                    new_acc(bt)
+                for ci in range(2):
+                    c = 2 * half + ci
+                    wc, ws = q[ci]
+                    nc.tensor.matmul_mx(
+                        out=acc[bt][:],
+                        lhsT=acodes[:, c, bt * 128:(bt + 1) * 128].bitcast(FP8X4),
+                        lhsT_scale=ascales[:, c, bt * 128:(bt + 1) * 128],
+                        rhs=wc[:].bitcast(FP8X4),
+                        rhs_scale=ws[:],
+                        start=(half == 0 and ci == 0),
+                        stop=(half == 1 and ci == 1),
+                    )
+
+        def bias_matmuls(r0):
+            for r in range(r0, r0 + 4):
+                bt = r % 4
+                new_acc(bt)
+                nc.tensor.matmul(
+                    out=acc[bt][:],
+                    lhsT=ident_b[:, r:r + 1].to_broadcast([128, 128]),
+                    rhs=bz[:],
+                    start=True,
+                    stop=True,
+                )
+                dst = bias_sb[:, r // 2, (r % 2) * 512:(r % 2) * 512 + 512]
+                if r % 2 == 0:
+                    nc.scalar.copy(out=dst, in_=acc[bt][:])
+                else:
+                    nc.vector.tensor_copy(out=dst, in_=acc[bt][:])
+
+        pre_of = {}
+        c_of = {}
+        out_h = out_0.rearrange("(p t) h -> p t h", t=4)
+        out_c = out_1.rearrange("(p t) h -> p t h", t=4)
+
+        def bias_add(j, bt):
+            nc.vector.tensor_tensor(
+                out=pre_of[j][:, bt, :].rearrange("p (g c) -> p g c", g=4),
+                in0=acc[bt][:].rearrange("p (g c) -> p g c", g=4),
+                in1=bias_sb[:, :, j * 128:(j + 1) * 128],
+                op=ALU.add,
+            )
+
+        def gate_acts(j, b0, b1):
+            pre = pre_of[j]
+            nc.scalar.activation(out=pre[:, b0:b1, 0:384], in_=pre[:, b0:b1, 0:384], func=ACT.Sigmoid)
+            nc.scalar.activation(out=pre[:, b0:b1, 384:512], in_=pre[:, b0:b1, 384:512], func=ACT.Tanh)
+
+        def new_cell(eng, j, b0, b1):
+            pre = pre_of[j]
+            gi = pre[:, b0:b1, 0:128]
+            gf = pre[:, b0:b1, 128:256]
+            gg = pre[:, b0:b1, 384:512]
+            eng.tensor_tensor(out=gf, in0=gf, in1=cell_sb[:, b0:b1, j * 128:(j + 1) * 128], op=ALU.mult)
+            eng.tensor_tensor(out=gi, in0=gi, in1=gg, op=ALU.mult)
+            eng.tensor_tensor(out=c_of[j][:, b0:b1, :], in0=gf, in1=gi, op=ALU.add)
+
+        def tanh_cell(j, b0, b1):
+            nc.scalar.activation(out=pre_of[j][:, b0:b1, 384:512], in_=c_of[j][:, b0:b1, :], func=ACT.Tanh)
+
+        h_of = {}
+
+        def new_hidden(eng, j, b0, b1):
+            pre = pre_of[j]
+            eng.tensor_tensor(
+                out=h_of[j][:, b0:b1, :], in0=pre[:, b0:b1, 256:384], in1=pre[:, b0:b1, 384:512], op=ALU.mult
+            )
+
+        def store(dram, t, j, b0, b1):
+            nc.sync.dma_start(out=dram[:, b0:b1, j * 128:(j + 1) * 128], in_=t[:, b0:b1, :])
+
+        def w_chunks(w):
+            j = w // 2
+            return chunks_of([raw_w[(j, 0)], raw_w[(j, 1)], raw_w[(j, 2)]], w % 2)
+
+        SV = "svsv"
+        g_a0 = evacuate(transposes(chunks_of(raw_act, 0)), SV)
+        bias_matmuls(0)
+        g_w = evacuate(transposes(w_chunks(0)), SV)
+        quantise_act(g_a0, 0)
+        bias_matmuls(4)
+        g_a1 = evacuate(transposes(chunks_of(raw_act, 1)), SV)
+        q_cur = quantise_w(g_w)
+        mx_passes(0, q_cur)
+        quantise_act(g_a1, 1)
+        g_w = evacuate(transposes(w_chunks(1)), SV)
+        for s in range(3):
+            load_w(NB_RAW, s)
+        q_cur = quantise_w(g_w)
+
+        n_units = 2 * N_BLOCKS
+        for w in range(1, n_units):
+            nxt = w + 1
+            if nxt < n_units:
+                g_w = evacuate(transposes(w_chunks(nxt)), "ssss" if nxt % 2 == 0 else SV)
+                if nxt % 2 == 1 and nxt // 2 + NB_RAW < N_BLOCKS:
+                    for s in range(3):
+                        load_w(nxt // 2 + NB_RAW, s)
+            if w % 2 == 0:
+                j = w // 2 - 1
+                gate_acts(j, 0, 4)
+                c_of[j] = outp.tile([128, 4, 128], F32, name="co", tag="co")
+                new_cell(nc.gpsimd, j, 0, 4)
+                store(out_c, c_of[j], j, 0, 4)
+            elif w >= 3:
+                j = (w - 3) // 2
+                tanh_cell(j, 0, 4)
+                h_of[j] = outp.tile([128, 4, 128], F32, name="ho", tag="ho")
+                new_hidden(nc.gpsimd, j, 0, 4)
+                store(out_h, h_of[j], j, 0, 4)
+            mx_passes(w % 2, q_cur)
+            if nxt < n_units:
+                q_cur = quantise_w(g_w)
+            if w % 2 == 1 and w < n_units - 1:
+                j = w // 2
+                pre_of[j] = prep.tile([128, 4, 512], F32, name="pre", tag="pre")
+                for bt in range(4):
+                    bias_add(j, bt)
+
+        j = N_BLOCKS - 1
+        pre_of[j] = prep.tile([128, 4, 512], F32, name="pre", tag="pre")
+        c_of[j] = outp.tile([128, 4, 128], F32, name="co", tag="co")
+        h_of[j] = outp.tile([128, 4, 128], F32, name="ho", tag="ho")
+        for bt in range(4):
+            bias_add(j, bt)
+            gate_acts(j, bt, bt + 1)
+        new_cell(nc.gpsimd, j, 0, 2)
+        tanh_cell(j, 0, 2)
+        store(out_c, c_of[j], j, 0, 2)
+        new_hidden(nc.gpsimd, j, 0, 2)
+        store(out_h, h_of[j], j, 0, 2)
+        new_cell(nc.vector, j, 2, 3)
+        new_cell(nc.vector, j, 3, 4)
+        tanh_cell(j, 2, 4)
+        store(out_c, c_of[j], j, 2, 4)
+        new_hidden(nc.vector, j, 2, 4)
+        store(out_h, h_of[j], j, 2, 4)

@@ -15,6 +15,8 @@ FLOPS = 2 * 512 * 2048 * 4096
 
 NB_RAW = 5
 N_BLOCKS = 8
+CFG = {"ev": "ssssssss", "ew": ["vvvv","vvvv","vvvv","vvvv","vvvv","vvvv","vvvv","vvvv"], "cuts": [[[0,4]],[[0,4]],[[0,4]],[[0,4]],[[0,4]],[[0,4]],[[0,2],[2,4]],[[0,1],[1,2],[2,3],[3,4]]], "stores": [[[0,4]],[[0,4]],[[0,4]],[[0,4]],[[0,4]],[[0,4]],[[0,4]],[[0,2],[2,4]]]}
+ORDER = [0, 1, 2, 5, 3, 7, 6, 9, 11, 8, 10, 13, 14, 12, 15, 16, 18, 19, 4, 20, 23, 25, 21, 24, 27, 29, 26, 28, 31, 32, 30, 33, 34, 36, 17, 37, 38, 41, 22, 42, 43, 46, 39, 47, 44, 48, 49, 35, 40, 50, 51, 45, 52, 53, 54, 55, 56, 59, 57, 60, 61, 65, 58, 66, 67, 70, 62, 72, 68, 71, 75, 73, 76, 77, 63, 78, 69, 79, 80, 74, 81, 82, 83, 87, 84, 88, 89, 92, 85, 93, 90, 107, 86, 108, 94, 112, 91, 95, 113, 117, 109, 96, 118, 122, 110, 123, 128, 114, 111, 129, 115, 130, 131, 119, 133, 116, 134, 120, 135, 132, 136, 138, 124, 121, 139, 140, 125, 137, 141, 143, 98, 126, 144, 145, 64, 142, 146, 157, 147, 158, 99, 162, 100, 163, 159, 167, 101, 160, 168, 172, 102, 164, 173, 177, 161, 165, 178, 179, 169, 166, 180, 97, 182, 170, 181, 183, 184, 174, 171, 185, 187, 175, 188, 186, 189, 103, 190, 176, 192, 148, 193, 191, 194, 195, 104, 206, 207, 196, 208, 211, 105, 212, 150, 106, 209, 216, 127, 217, 213, 210, 221, 214, 222, 226, 218, 215, 227, 228, 219, 229, 231, 223, 230, 232, 233, 224, 220, 234, 236, 149, 237, 235, 238, 197, 239, 225, 241, 242, 240, 243, 244, 151, 255, 198, 256, 245, 260, 257, 261, 152, 258, 265, 199, 266, 155, 262, 270, 259, 271, 263, 275, 200, 267, 276, 277, 264, 268, 278, 280, 201, 272, 281, 282, 279, 283, 273, 285, 286, 153, 284, 287, 288, 202, 269, 290, 291, 246, 289, 292, 293, 274, 304, 305, 294, 309, 306, 310, 154, 314, 307, 203, 315, 156, 204, 311, 319, 308, 320, 205, 312, 324, 248, 325, 316, 326, 313, 327, 317, 329, 328, 330, 321, 331, 318, 332, 322, 334, 335, 333, 247, 336, 337, 323, 295, 339, 340, 338, 341, 342, 249, 353, 296, 354, 343, 358, 355, 359, 250, 363, 356, 297, 364, 253, 368, 360, 357, 369, 361, 373, 298, 374, 365, 375, 362, 376, 366, 378, 299, 379, 370, 380, 377, 381, 371, 383, 384, 382, 251, 385, 386, 367, 300, 388, 389, 387, 344, 390, 391, 372, 409, 410, 392, 411, 412, 345, 252, 414, 415, 393, 416, 413, 254, 302, 417, 419, 301, 420, 394, 421, 400, 418, 303, 422, 424, 423, 425, 401, 426, 429, 427, 346, 430, 436, 428, 437, 443, 347, 444, 450, 348, 451, 395, 349, 351, 396, 397, 350, 398, 399, 352, 402, 403, 404, 431, 405, 407, 432, 433, 406, 434, 435, 408, 438, 439, 440, 445, 441, 457, 446, 442, 447, 458, 452, 448, 453, 449, 454, 455, 459, 456, 460]
 
 
 def tile_structuredlstmcell_kernel(
@@ -33,14 +35,15 @@ def tile_structuredlstmcell_kernel(
     k_src = [512, 512, 1024]
     biases = [b_pi, b_pf, b_po, b_pg]
     acts = [P, ext_input, hidden]
+    eng_of = {"v": nc.vector, "g": nc.gpsimd}
 
     with ExitStack() as ctx:
         ctx.enter_context(tc.manual_schedule())
         const = ctx.enter_context(tc.tile_pool(name="const", bufs=1))
         rawp = ctx.enter_context(tc.tile_pool(name="rawp", bufs=NB_RAW))
-        gpool = ctx.enter_context(tc.tile_pool(name="gpool", bufs=4))
-        cpool = ctx.enter_context(tc.tile_pool(name="cpool", bufs=6))
-        prep = ctx.enter_context(tc.tile_pool(name="prep", bufs=3))
+        gpool = ctx.enter_context(tc.tile_pool(name="gpool", bufs=8))
+        cpool = ctx.enter_context(tc.tile_pool(name="cpool", bufs=8))
+        prep = ctx.enter_context(tc.tile_pool(name="prep", bufs=4))
         outp = ctx.enter_context(tc.tile_pool(name="outp", bufs=3))
         psum = ctx.enter_context(tc.psum_pool(name="psum", bufs=1))
 
@@ -68,10 +71,7 @@ def tile_structuredlstmcell_kernel(
         ascales = const.tile([128, 4, 512], U8, name="ascales", align_bytes=64)
 
         def load_act(s):
-            nc.sync.dma_start(
-                out=raw_act[s][:],
-                in_=acts[s].rearrange("(p t) k -> p (t k)", t=4),
-            )
+            nc.sync.dma_start(out=raw_act[s][:], in_=acts[s].rearrange("(p t) k -> p (t k)", t=4))
 
         raw_w = {}
 
@@ -79,230 +79,243 @@ def tile_structuredlstmcell_kernel(
             k = k_src[s]
             t = rawp.tile([128, 4 * k], BF16, name="rw%d" % s, tag="rw%d" % s)
             for gi in range(4):
-                nc.sync.dma_start(
-                    out=t[:, gi * k:(gi + 1) * k],
-                    in_=w_src[s][gi][j * 128:(j + 1) * 128, :],
-                )
+                nc.sync.dma_start(out=t[:, gi * k:(gi + 1) * k], in_=w_src[s][gi][j * 128:(j + 1) * 128, :])
             raw_w[(j, s)] = t
 
+        def load_cell():
+            nc.sync.dma_start(
+                out=cell_sb[:].rearrange("p t h -> p (t h)"), in_=cell.rearrange("(p t) h -> p (t h)", t=4)
+            )
+
         load_act(0)
-        load_act(1)
         load_w(0, 0)
+        load_act(1)
         load_w(0, 1)
         load_act(2)
         load_w(0, 2)
-        load_w(1, 0)
-        load_w(1, 1)
-        load_w(1, 2)
-        nc.sync.dma_start(
-            out=cell_sb[:].rearrange("p t h -> p (t h)"),
-            in_=cell.rearrange("(p t) h -> p (t h)", t=4),
-        )
+        for s in range(3):
+            load_w(1, s)
+        load_cell()
         for j in range(2, NB_RAW):
             for s in range(3):
                 load_w(j, s)
 
-        def chunks_of(tiles, half):
-            if half == 0:
-                return [(tiles[0], 256, 0), (tiles[1], 256, 0)]
-            return [(tiles[2], 512, 0), (tiles[2], 512, 256)]
+        free_banks = list(range(8))
 
-        def transposes(chunks):
-            banks = []
-            for ci in range(2):
-                raw, kw, off = chunks[ci]
-                rw = raw[:].bitcast(F32)
-                for a in range(2):
-                    slot = 2 * ci + a
-                    xt = psum.tile([128, 2, 256], F32, name="xt%d" % slot, tag="xt%d" % slot)
-                    for g2 in range(2):
-                        for u in range(2):
-                            col = (2 * a + g2) * kw + off + 128 * u
-                            nc.tensor.transpose(
-                                xt[:, u, g2 * 128:(g2 + 1) * 128],
-                                rw[:, col:col + 128],
-                                ident_f[:],
-                            )
-                    banks.append(xt)
-            return banks
+        def bank_tile(shape):
+            b = free_banks.pop(0)
+            t = psum.tile(shape, F32, name="bk%d" % b, tag="bk%d" % b)
+            return b, t
 
-        def evacuate(banks, engines):
-            grps = []
-            for ci in range(2):
-                grp = gpool.tile([128, 2048], BF16, name="grp", tag="grp", align_bytes=64)
-                gw = grp[:].bitcast(F32)
-                for a in range(2):
-                    slot = 2 * ci + a
-                    dst = gw[:, a * 512:(a + 1) * 512].rearrange("p (n u) -> p n u", u=2)
-                    src = banks[slot][:].rearrange("p u n -> p n u")
-                    if engines[slot] == "s":
-                        nc.scalar.copy(out=dst, in_=src)
-                    else:
-                        nc.vector.tensor_copy(out=dst, in_=src)
-                grps.append(grp)
-            return grps
+        tasks = []
 
-        def quantise_act(grps, half):
-            for ci in range(2):
-                c = 2 * half + ci
-                nc.vector.quantize_mx(
-                    out=acodes[:, c, :].bitcast(FP8X4),
-                    scales=ascales[:, c, :],
-                    in_=grps[ci][:],
-                )
+        def task(fn, *args):
+            tasks.append((fn, args))
 
-        def quantise_w(grps):
-            res = []
-            for ci in range(2):
-                wc = cpool.tile([128, 512], U32, name="wc", tag="wc", align_bytes=64)
-                ws = cpool.tile([128, 512], U8, name="ws", tag="ws", align_bytes=64)
-                nc.vector.quantize_mx(out=wc[:].bitcast(FP8X4), scales=ws[:], in_=grps[ci][:])
-                res.append((wc, ws))
-            return res
-
-        acc = [None, None, None, None]
-
-        def new_acc(bt):
-            acc[bt] = psum.tile([128, 512], F32, name="acc%d" % bt, tag="acc%d" % bt)
-
-        def mx_passes(half, q):
-            for bt in range(4):
-                if half == 0:
-                    new_acc(bt)
-                for ci in range(2):
-                    c = 2 * half + ci
-                    wc, ws = q[ci]
-                    nc.tensor.matmul_mx(
-                        out=acc[bt][:],
-                        lhsT=acodes[:, c, bt * 128:(bt + 1) * 128].bitcast(FP8X4),
-                        lhsT_scale=ascales[:, c, bt * 128:(bt + 1) * 128],
-                        rhs=wc[:].bitcast(FP8X4),
-                        rhs_scale=ws[:],
-                        start=(half == 0 and ci == 0),
-                        stop=(half == 1 and ci == 1),
-                    )
-
-        def bias_matmuls(r0):
-            for r in range(r0, r0 + 4):
-                bt = r % 4
-                new_acc(bt)
-                nc.tensor.matmul(
-                    out=acc[bt][:],
-                    lhsT=ident_b[:, r:r + 1].to_broadcast([128, 128]),
-                    rhs=bz[:],
-                    start=True,
-                    stop=True,
-                )
-                dst = bias_sb[:, r // 2, (r % 2) * 512:(r % 2) * 512 + 512]
-                if r % 2 == 0:
-                    nc.scalar.copy(out=dst, in_=acc[bt][:])
-                else:
-                    nc.vector.tensor_copy(out=dst, in_=acc[bt][:])
-
+        grp_of = {}
+        xt_of = {}
+        q_of = {}
+        acc = {}
         pre_of = {}
         c_of = {}
+        h_of = {}
         out_h = out_0.rearrange("(p t) h -> p t h", t=4)
         out_c = out_1.rearrange("(p t) h -> p t h", t=4)
 
+        def tiles_of(j):
+            if j < 0:
+                return raw_act
+            return [raw_w[(j, 0)], raw_w[(j, 1)], raw_w[(j, 2)]]
+
+        def t_bank(j, c, a):
+            tl = tiles_of(j)
+            if c < 2:
+                raw, kw, off = tl[c], 256, 0
+            else:
+                raw, kw, off = tl[2], 512, 256 * (c - 2)
+            rw = raw[:].bitcast(F32)
+            if a == 0:
+                grp_of[(j, c)] = gpool.tile([128, 2048], BF16, name="grp", tag="grp", align_bytes=64)
+            b, xt = bank_tile([128, 2, 256])
+            for g2 in range(2):
+                for u in range(2):
+                    col = (2 * a + g2) * kw + off + 128 * u
+                    nc.tensor.transpose(xt[:, u, g2 * 128:(g2 + 1) * 128], rw[:, col:col + 128], ident_f[:])
+            xt_of[(j, c, a)] = (b, xt)
+
+        def e_bank(j, c, a, e):
+            b, xt = xt_of[(j, c, a)]
+            gw = grp_of[(j, c)][:].bitcast(F32)
+            dst = gw[:, a * 512:(a + 1) * 512].rearrange("p (n u) -> p n u", u=2)
+            src = xt[:].rearrange("p u n -> p n u")
+            if e == "s":
+                nc.scalar.copy(out=dst, in_=src)
+            else:
+                nc.vector.tensor_copy(out=dst, in_=src)
+            free_banks.append(b)
+
+        def quant(j, c):
+            grp = grp_of[(j, c)]
+            if j < 0:
+                nc.vector.quantize_mx(out=acodes[:, c, :].bitcast(FP8X4), scales=ascales[:, c, :], in_=grp[:])
+            else:
+                wc = cpool.tile([128, 512], U32, name="wc", tag="wc", align_bytes=64)
+                ws = cpool.tile([128, 512], U8, name="ws", tag="ws", align_bytes=64)
+                nc.vector.quantize_mx(out=wc[:].bitcast(FP8X4), scales=ws[:], in_=grp[:])
+                q_of[(j, c)] = (wc, ws)
+
+        def mx_pass(j, bt, c):
+            if c == 0:
+                acc[(j, bt)] = bank_tile([128, 512])
+            wc, ws = q_of[(j, c)]
+            nc.tensor.matmul_mx(
+                out=acc[(j, bt)][1][:],
+                lhsT=acodes[:, c, bt * 128:(bt + 1) * 128].bitcast(FP8X4),
+                lhsT_scale=ascales[:, c, bt * 128:(bt + 1) * 128],
+                rhs=wc[:].bitcast(FP8X4),
+                rhs_scale=ws[:],
+                start=(c == 0),
+                stop=(c == 3),
+            )
+
+        bias_bank = {}
+
+        def bias_mm(r):
+            b, t = bank_tile([128, 512])
+            nc.tensor.matmul(
+                out=t[:], lhsT=ident_b[:, r:r + 1].to_broadcast([128, 128]), rhs=bz[:], start=True, stop=True
+            )
+            bias_bank[r] = (b, t)
+
+        def bias_ev(r):
+            b, t = bias_bank[r]
+            dst = bias_sb[:, r // 2, (r % 2) * 512:(r % 2) * 512 + 512]
+            if r % 2 == 0:
+                nc.scalar.copy(out=dst, in_=t[:])
+            else:
+                nc.vector.tensor_copy(out=dst, in_=t[:])
+            free_banks.append(b)
+
         def bias_add(j, bt):
+            if bt == 0:
+                pre_of[j] = prep.tile([128, 4, 512], F32, name="pre", tag="pre")
+            b, t = acc[(j, bt)]
             nc.vector.tensor_tensor(
                 out=pre_of[j][:, bt, :].rearrange("p (g c) -> p g c", g=4),
-                in0=acc[bt][:].rearrange("p (g c) -> p g c", g=4),
+                in0=t[:].rearrange("p (g c) -> p g c", g=4),
                 in1=bias_sb[:, :, j * 128:(j + 1) * 128],
                 op=ALU.add,
             )
+            free_banks.append(b)
 
-        def gate_acts(j, b0, b1):
+        def sig(j, b0, b1):
             pre = pre_of[j]
             nc.scalar.activation(out=pre[:, b0:b1, 0:384], in_=pre[:, b0:b1, 0:384], func=ACT.Sigmoid)
+
+        def tanh_g(j, b0, b1):
+            pre = pre_of[j]
             nc.scalar.activation(out=pre[:, b0:b1, 384:512], in_=pre[:, b0:b1, 384:512], func=ACT.Tanh)
 
-        def new_cell(eng, j, b0, b1):
-            pre = pre_of[j]
-            gi = pre[:, b0:b1, 0:128]
-            gf = pre[:, b0:b1, 128:256]
-            gg = pre[:, b0:b1, 384:512]
-            eng.tensor_tensor(out=gf, in0=gf, in1=cell_sb[:, b0:b1, j * 128:(j + 1) * 128], op=ALU.mult)
-            eng.tensor_tensor(out=gi, in0=gi, in1=gg, op=ALU.mult)
-            eng.tensor_tensor(out=c_of[j][:, b0:b1, :], in0=gf, in1=gi, op=ALU.add)
+        def mul_fc(e, j, b0, b1):
+            gf = pre_of[j][:, b0:b1, 128:256]
+            eng_of[e].tensor_tensor(out=gf, in0=gf, in1=cell_sb[:, b0:b1, j * 128:(j + 1) * 128], op=ALU.mult)
+
+        def mul_ig(e, j, b0, b1):
+            gi = pre_of[j][:, b0:b1, 0:128]
+            eng_of[e].tensor_tensor(out=gi, in0=gi, in1=pre_of[j][:, b0:b1, 384:512], op=ALU.mult)
+
+        def add_c(e, j, b0, b1):
+            if j not in c_of:
+                c_of[j] = outp.tile([128, 4, 128], F32, name="co", tag="co")
+            eng_of[e].tensor_tensor(
+                out=c_of[j][:, b0:b1, :], in0=pre_of[j][:, b0:b1, 128:256], in1=pre_of[j][:, b0:b1, 0:128], op=ALU.add
+            )
 
         def tanh_cell(j, b0, b1):
             nc.scalar.activation(out=pre_of[j][:, b0:b1, 384:512], in_=c_of[j][:, b0:b1, :], func=ACT.Tanh)
 
-        h_of = {}
-
-        def new_hidden(eng, j, b0, b1):
-            pre = pre_of[j]
-            eng.tensor_tensor(
-                out=h_of[j][:, b0:b1, :], in0=pre[:, b0:b1, 256:384], in1=pre[:, b0:b1, 384:512], op=ALU.mult
+        def mul_h(e, j, b0, b1):
+            if j not in h_of:
+                h_of[j] = outp.tile([128, 4, 128], F32, name="ho", tag="ho")
+            eng_of[e].tensor_tensor(
+                out=h_of[j][:, b0:b1, :], in0=pre_of[j][:, b0:b1, 256:384], in1=pre_of[j][:, b0:b1, 384:512], op=ALU.mult
             )
 
-        def store(dram, t, j, b0, b1):
-            nc.sync.dma_start(out=dram[:, b0:b1, j * 128:(j + 1) * 128], in_=t[:, b0:b1, :])
+        def store_c(j, b0, b1):
+            nc.sync.dma_start(out=out_c[:, b0:b1, j * 128:(j + 1) * 128], in_=c_of[j][:, b0:b1, :])
 
-        def w_chunks(w):
-            j = w // 2
-            return chunks_of([raw_w[(j, 0)], raw_w[(j, 1)], raw_w[(j, 2)]], w % 2)
+        def store_h(j, b0, b1):
+            nc.sync.dma_start(out=out_h[:, b0:b1, j * 128:(j + 1) * 128], in_=h_of[j][:, b0:b1, :])
 
-        SV = "svsv"
-        g_a0 = evacuate(transposes(chunks_of(raw_act, 0)), SV)
-        bias_matmuls(0)
-        g_w = evacuate(transposes(w_chunks(0)), SV)
-        quantise_act(g_a0, 0)
-        bias_matmuls(4)
-        g_a1 = evacuate(transposes(chunks_of(raw_act, 1)), SV)
-        q_cur = quantise_w(g_w)
-        mx_passes(0, q_cur)
-        quantise_act(g_a1, 1)
-        g_w = evacuate(transposes(w_chunks(1)), SV)
-        for s in range(3):
-            load_w(NB_RAW, s)
-        q_cur = quantise_w(g_w)
+        def load_block(j):
+            for s in range(3):
+                load_w(j, s)
 
-        n_units = 2 * N_BLOCKS
-        for w in range(1, n_units):
-            nxt = w + 1
-            if nxt < n_units:
-                g_w = evacuate(transposes(w_chunks(nxt)), "ssss" if nxt % 2 == 0 else SV)
-                if nxt % 2 == 1 and nxt // 2 + NB_RAW < N_BLOCKS:
-                    for s in range(3):
-                        load_w(nxt // 2 + NB_RAW, s)
-            if w % 2 == 0:
-                j = w // 2 - 1
-                gate_acts(j, 0, 4)
-                c_of[j] = outp.tile([128, 4, 128], F32, name="co", tag="co")
-                new_cell(nc.gpsimd, j, 0, 4)
-                store(out_c, c_of[j], j, 0, 4)
-            elif w >= 3:
-                j = (w - 3) // 2
-                tanh_cell(j, 0, 4)
-                h_of[j] = outp.tile([128, 4, 128], F32, name="ho", tag="ho")
-                new_hidden(nc.gpsimd, j, 0, 4)
-                store(out_h, h_of[j], j, 0, 4)
-            mx_passes(w % 2, q_cur)
-            if nxt < n_units:
-                q_cur = quantise_w(g_w)
-            if w % 2 == 1 and w < n_units - 1:
-                j = w // 2
-                pre_of[j] = prep.tile([128, 4, 512], F32, name="pre", tag="pre")
-                for bt in range(4):
-                    bias_add(j, bt)
+        def chunk(j, c, ev):
+            task(t_bank, j, c, 0)
+            task(t_bank, j, c, 1)
+            task(e_bank, j, c, 0, ev[0])
+            task(e_bank, j, c, 1, ev[1])
+            task(quant, j, c)
 
-        j = N_BLOCKS - 1
-        pre_of[j] = prep.tile([128, 4, 512], F32, name="pre", tag="pre")
-        c_of[j] = outp.tile([128, 4, 128], F32, name="co", tag="co")
-        h_of[j] = outp.tile([128, 4, 128], F32, name="ho", tag="ho")
+        def epilogue(j):
+            cuts = CFG["cuts"][j]
+            e = CFG["ew"][j]
+            for b0, b1 in cuts:
+                task(sig, j, b0, b1)
+                task(tanh_g, j, b0, b1)
+                task(mul_fc, e[0], j, b0, b1)
+                task(mul_ig, e[1], j, b0, b1)
+                task(add_c, e[2], j, b0, b1)
+                task(tanh_cell, j, b0, b1)
+                task(mul_h, e[3], j, b0, b1)
+            for b0, b1 in CFG["stores"][j]:
+                task(store_c, j, b0, b1)
+                task(store_h, j, b0, b1)
+
+        chunk(-1, 0, "sv")
+        for r in range(4):
+            task(bias_mm, r)
+            task(bias_ev, r)
+        chunk(0, 0, "sv")
+        chunk(-1, 1, "sv")
+        for r in range(4, 8):
+            task(bias_mm, r)
+            task(bias_ev, r)
+        chunk(0, 1, "sv")
+        chunk(-1, 2, "sv")
+        chunk(-1, 3, "sv")
+        for c in (0, 1):
+            for bt in range(4):
+                task(mx_pass, 0, bt, c)
+        chunk(0, 2, "sv")
+        chunk(0, 3, "sv")
+        task(load_block, NB_RAW)
+        chunk(1, 0, "sv")
+        chunk(1, 1, "sv")
+        for c in (2, 3):
+            for bt in range(4):
+                task(mx_pass, 0, bt, c)
         for bt in range(4):
-            bias_add(j, bt)
-            gate_acts(j, bt, bt + 1)
-        new_cell(nc.gpsimd, j, 0, 2)
-        tanh_cell(j, 0, 2)
-        store(out_c, c_of[j], j, 0, 2)
-        new_hidden(nc.gpsimd, j, 0, 2)
-        store(out_h, h_of[j], j, 0, 2)
-        new_cell(nc.vector, j, 2, 3)
-        new_cell(nc.vector, j, 3, 4)
-        tanh_cell(j, 2, 4)
-        store(out_c, c_of[j], j, 2, 4)
-        new_hidden(nc.vector, j, 2, 4)
-        store(out_h, h_of[j], j, 2, 4)
+            task(bias_add, 0, bt)
+        chunk(1, 2, CFG["ev"][4:6])
+        chunk(1, 3, CFG["ev"][6:8])
+        task(load_block, NB_RAW + 1)
+        epilogue(0)
+        for p in range(1, N_BLOCKS):
+            nxt = p + 1
+            if nxt < N_BLOCKS:
+                for c in range(4):
+                    chunk(nxt, c, CFG["ev"][2 * c:2 * c + 2])
+                if nxt + NB_RAW < N_BLOCKS:
+                    task(load_block, nxt + NB_RAW)
+            for bt in range(4):
+                for c in range(4):
+                    task(mx_pass, p, bt, c)
+                task(bias_add, p, bt)
+            epilogue(p)
+
+        order = ORDER if ORDER else list(range(len(tasks)))
+        for i in order:
+            fn, args = tasks[i]
+            fn(*args)

@@ -15,8 +15,8 @@ FLOPS = 2 * 512 * 2048 * 4096
 
 NB_RAW = 5
 N_BLOCKS = 8
-CFG = {"ev": "ssssssss", "ew": ["vvvv","vvvv","vvvv","vvvv","vvvv","vvvv","vvvv","vvvv"], "cuts": [[[0,4]],[[0,4]],[[0,4]],[[0,4]],[[0,4]],[[0,4]],[[0,2],[2,4]],[[0,1],[1,2],[2,3],[3,4]]], "stores": [[[0,4]],[[0,4]],[[0,4]],[[0,4]],[[0,4]],[[0,4]],[[0,4]],[[0,2],[2,4]]]}
-ORDER = [0, 1, 2, 5, 3, 7, 6, 9, 11, 8, 10, 13, 14, 12, 15, 16, 18, 19, 4, 20, 23, 25, 21, 24, 27, 29, 26, 28, 31, 32, 30, 33, 34, 36, 17, 37, 38, 41, 22, 42, 43, 46, 39, 47, 44, 48, 49, 35, 40, 50, 51, 45, 52, 53, 54, 55, 56, 59, 57, 60, 61, 65, 58, 66, 67, 70, 62, 72, 68, 71, 75, 73, 76, 77, 63, 78, 69, 79, 80, 74, 81, 82, 83, 87, 84, 88, 89, 92, 85, 93, 90, 107, 86, 108, 94, 112, 91, 95, 113, 117, 109, 96, 118, 122, 110, 123, 128, 114, 111, 129, 115, 130, 131, 119, 133, 116, 134, 120, 135, 132, 136, 138, 124, 121, 139, 140, 125, 137, 141, 143, 98, 126, 144, 145, 64, 142, 146, 157, 147, 158, 99, 162, 100, 163, 159, 167, 101, 160, 168, 172, 102, 164, 173, 177, 161, 165, 178, 179, 169, 166, 180, 97, 182, 170, 181, 183, 184, 174, 171, 185, 187, 175, 188, 186, 189, 103, 190, 176, 192, 148, 193, 191, 194, 195, 104, 206, 207, 196, 208, 211, 105, 212, 150, 106, 209, 216, 127, 217, 213, 210, 221, 214, 222, 226, 218, 215, 227, 228, 219, 229, 231, 223, 230, 232, 233, 224, 220, 234, 236, 149, 237, 235, 238, 197, 239, 225, 241, 242, 240, 243, 244, 151, 255, 198, 256, 245, 260, 257, 261, 152, 258, 265, 199, 266, 155, 262, 270, 259, 271, 263, 275, 200, 267, 276, 277, 264, 268, 278, 280, 201, 272, 281, 282, 279, 283, 273, 285, 286, 153, 284, 287, 288, 202, 269, 290, 291, 246, 289, 292, 293, 274, 304, 305, 294, 309, 306, 310, 154, 314, 307, 203, 315, 156, 204, 311, 319, 308, 320, 205, 312, 324, 248, 325, 316, 326, 313, 327, 317, 329, 328, 330, 321, 331, 318, 332, 322, 334, 335, 333, 247, 336, 337, 323, 295, 339, 340, 338, 341, 342, 249, 353, 296, 354, 343, 358, 355, 359, 250, 363, 356, 297, 364, 253, 368, 360, 357, 369, 361, 373, 298, 374, 365, 375, 362, 376, 366, 378, 299, 379, 370, 380, 377, 381, 371, 383, 384, 382, 251, 385, 386, 367, 300, 388, 389, 387, 344, 390, 391, 372, 409, 410, 392, 411, 412, 345, 252, 414, 415, 393, 416, 413, 254, 302, 417, 419, 301, 420, 394, 421, 400, 418, 303, 422, 424, 423, 425, 401, 426, 429, 427, 346, 430, 436, 428, 437, 443, 347, 444, 450, 348, 451, 395, 349, 351, 396, 397, 350, 398, 399, 352, 402, 403, 404, 431, 405, 407, 432, 433, 406, 434, 435, 408, 438, 439, 440, 445, 441, 457, 446, 442, 447, 458, 452, 448, 453, 449, 454, 455, 459, 456, 460]
+CFG = {"ev":"ssssssss","pev":"svsvsvsvssssssssssss","ew":["vvvv","vvvv","vvvv","vvvv","vvvv","vvvv","vvvv","vvvv"],"cuts":[[[0,4]],[[0,4]],[[0,4]],[[0,4]],[[0,4]],[[0,4]],[[0,2],[2,4]],[[0,1],[1,2],[2,3],[3,4]]],"stores":[[[0,4]],[[0,4]],[[0,4]],[[0,4]],[[0,4]],[[0,4]],[[0,4]],[[0,2],[2,4]]],"run":2}
+ORDER = [0, 1, 2, 5, 3, 7, 6, 4, 9, 8, 11, 10, 13, 12, 14, 15, 18, 16, 19, 20, 23, 17, 25, 24, 27, 21, 29, 28, 31, 26, 32, 33, 36, 30, 37, 38, 41, 34, 42, 39, 46, 22, 43, 47, 48, 35, 49, 44, 40, 50, 51, 45, 52, 53, 54, 55, 56, 59, 60, 57, 65, 61, 58, 66, 62, 70, 67, 63, 71, 75, 68, 76, 77, 72, 69, 78, 79, 73, 80, 83, 81, 82, 84, 87, 88, 85, 89, 92, 93, 90, 86, 107, 108, 94, 74, 112, 95, 113, 91, 109, 117, 96, 110, 118, 114, 111, 119, 115, 120, 122, 98, 116, 123, 124, 121, 125, 127, 126, 128, 99, 132, 100, 133, 129, 138, 101, 130, 139, 140, 102, 64, 134, 141, 143, 131, 144, 135, 145, 142, 146, 103, 157, 136, 158, 159, 147, 162, 163, 160, 104, 167, 164, 168, 161, 169, 170, 165, 172, 171, 173, 97, 148, 174, 166, 175, 177, 176, 178, 182, 179, 150, 183, 187, 180, 188, 184, 181, 189, 190, 185, 192, 191, 193, 149, 194, 186, 195, 105, 206, 106, 137, 196, 207, 208, 211, 151, 212, 209, 216, 152, 213, 217, 218, 210, 219, 214, 221, 220, 222, 153, 223, 215, 224, 197, 226, 225, 227, 231, 154, 232, 236, 228, 199, 237, 155, 229, 238, 156, 239, 233, 230, 241, 242, 234, 243, 240, 244, 198, 255, 235, 256, 257, 245, 260, 261, 258, 200, 265, 262, 266, 259, 267, 268, 263, 201, 270, 271, 246, 269, 204, 272, 273, 264, 275, 276, 274, 280, 277, 281, 248, 285, 278, 286, 282, 279, 287, 288, 283, 290, 289, 291, 202, 292, 284, 293, 247, 304, 294, 305, 306, 309, 203, 310, 307, 314, 249, 205, 311, 315, 316, 308, 317, 312, 319, 250, 320, 295, 321, 318, 253, 322, 324, 323, 325, 329, 313, 326, 330, 334, 327, 297, 335, 331, 328, 336, 337, 332, 339, 338, 340, 251, 341, 333, 342, 296, 353, 343, 354, 355, 358, 252, 359, 356, 363, 298, 254, 360, 364, 365, 357, 366, 361, 368, 299, 369, 344, 370, 367, 302, 371, 373, 372, 374, 378, 362, 375, 379, 383, 376, 346, 384, 380, 377, 385, 386, 381, 388, 387, 389, 300, 390, 382, 391, 345, 409, 410, 392, 393, 411, 412, 301, 414, 394, 415, 413, 303, 416, 400, 417, 347, 419, 420, 401, 418, 421, 429, 422, 430, 424, 348, 436, 425, 426, 437, 423, 351, 349, 427, 395, 443, 428, 444, 350, 450, 451, 396, 352, 397, 402, 398, 403, 399, 404, 431, 405, 407, 432, 433, 406, 434, 435, 408, 438, 439, 440, 445, 441, 457, 446, 442, 447, 458, 452, 448, 453, 449, 454, 455, 459, 456, 460]
 
 
 def tile_structuredlstmcell_kernel(
@@ -273,26 +273,26 @@ def tile_structuredlstmcell_kernel(
                 task(store_c, j, b0, b1)
                 task(store_h, j, b0, b1)
 
-        chunk(-1, 0, "sv")
+        chunk(-1, 0, CFG["pev"][0:2])
         for r in range(4):
             task(bias_mm, r)
             task(bias_ev, r)
-        chunk(0, 0, "sv")
-        chunk(-1, 1, "sv")
+        chunk(0, 0, CFG["pev"][2:4])
+        chunk(-1, 1, CFG["pev"][4:6])
         for r in range(4, 8):
             task(bias_mm, r)
             task(bias_ev, r)
-        chunk(0, 1, "sv")
-        chunk(-1, 2, "sv")
-        chunk(-1, 3, "sv")
+        chunk(0, 1, CFG["pev"][6:8])
+        chunk(-1, 2, CFG["pev"][8:10])
+        chunk(-1, 3, CFG["pev"][10:12])
         for c in (0, 1):
             for bt in range(4):
                 task(mx_pass, 0, bt, c)
-        chunk(0, 2, "sv")
-        chunk(0, 3, "sv")
+        chunk(0, 2, CFG["pev"][12:14])
+        chunk(0, 3, CFG["pev"][14:16])
         task(load_block, NB_RAW)
-        chunk(1, 0, "sv")
-        chunk(1, 1, "sv")
+        chunk(1, 0, CFG["pev"][16:18])
+        chunk(1, 1, CFG["pev"][18:20])
         for c in (2, 3):
             for bt in range(4):
                 task(mx_pass, 0, bt, c)
@@ -304,15 +304,17 @@ def tile_structuredlstmcell_kernel(
         epilogue(0)
         for p in range(1, N_BLOCKS):
             nxt = p + 1
-            if nxt < N_BLOCKS:
-                for c in range(4):
-                    chunk(nxt, c, CFG["ev"][2 * c:2 * c + 2])
-                if nxt + NB_RAW < N_BLOCKS:
-                    task(load_block, nxt + NB_RAW)
-            for bt in range(4):
-                for c in range(4):
-                    task(mx_pass, p, bt, c)
-                task(bias_add, p, bt)
+            per = CFG["run"]
+            for part in range(4 // per):
+                if nxt < N_BLOCKS:
+                    for c in range(part * per, (part + 1) * per):
+                        chunk(nxt, c, CFG["ev"][2 * c:2 * c + 2])
+                    if part == 4 // per - 1 and nxt + NB_RAW < N_BLOCKS:
+                        task(load_block, nxt + NB_RAW)
+                for bt in range(part * per, (part + 1) * per):
+                    for c in range(4):
+                        task(mx_pass, p, bt, c)
+                    task(bias_add, p, bt)
             epilogue(p)
 
         order = ORDER if ORDER else list(range(len(tasks)))

@@ -15,8 +15,9 @@ FLOPS = 2 * 512 * 2048 * 4096
 
 NB_RAW = 5
 N_BLOCKS = 8
-CFG = {"ev":"ssssssss","pev":"svsvsvsvssssssssssss","ew":["vvvv","vvvv","vvvv","vvvv","vvvv","vvvv","vvvv","vvvv"],"cuts":[[[0,4]],[[0,4]],[[0,4]],[[0,4]],[[0,4]],[[0,4]],[[0,2],[2,4]],[[0,1],[1,2],[2,3],[3,4]]],"stores":[[[0,4]],[[0,4]],[[0,4]],[[0,4]],[[0,4]],[[0,4]],[[0,4]],[[0,2],[2,4]]],"run":2}
-ORDER = [0, 1, 2, 5, 3, 7, 6, 4, 9, 8, 11, 10, 13, 12, 14, 15, 18, 16, 19, 20, 23, 17, 25, 24, 27, 21, 29, 28, 31, 26, 32, 33, 36, 30, 37, 38, 41, 34, 42, 39, 46, 22, 43, 47, 48, 35, 49, 44, 40, 50, 51, 45, 52, 53, 54, 55, 56, 59, 60, 57, 65, 61, 58, 66, 62, 70, 67, 63, 71, 75, 68, 76, 77, 72, 69, 78, 79, 73, 80, 83, 81, 82, 84, 87, 88, 85, 89, 92, 93, 90, 86, 107, 108, 94, 74, 112, 95, 113, 91, 109, 117, 96, 110, 118, 114, 111, 119, 115, 120, 122, 98, 116, 123, 124, 121, 125, 127, 126, 128, 99, 132, 100, 133, 129, 138, 101, 130, 139, 140, 102, 64, 134, 141, 143, 131, 144, 135, 145, 142, 146, 103, 157, 136, 158, 159, 147, 162, 163, 160, 104, 167, 164, 168, 161, 169, 170, 165, 172, 171, 173, 97, 148, 174, 166, 175, 177, 176, 178, 182, 179, 150, 183, 187, 180, 188, 184, 181, 189, 190, 185, 192, 191, 193, 149, 194, 186, 195, 105, 206, 106, 137, 196, 207, 208, 211, 151, 212, 209, 216, 152, 213, 217, 218, 210, 219, 214, 221, 220, 222, 153, 223, 215, 224, 197, 226, 225, 227, 231, 154, 232, 236, 228, 199, 237, 155, 229, 238, 156, 239, 233, 230, 241, 242, 234, 243, 240, 244, 198, 255, 235, 256, 257, 245, 260, 261, 258, 200, 265, 262, 266, 259, 267, 268, 263, 201, 270, 271, 246, 269, 204, 272, 273, 264, 275, 276, 274, 280, 277, 281, 248, 285, 278, 286, 282, 279, 287, 288, 283, 290, 289, 291, 202, 292, 284, 293, 247, 304, 294, 305, 306, 309, 203, 310, 307, 314, 249, 205, 311, 315, 316, 308, 317, 312, 319, 250, 320, 295, 321, 318, 253, 322, 324, 323, 325, 329, 313, 326, 330, 334, 327, 297, 335, 331, 328, 336, 337, 332, 339, 338, 340, 251, 341, 333, 342, 296, 353, 343, 354, 355, 358, 252, 359, 356, 363, 298, 254, 360, 364, 365, 357, 366, 361, 368, 299, 369, 344, 370, 367, 302, 371, 373, 372, 374, 378, 362, 375, 379, 383, 376, 346, 384, 380, 377, 385, 386, 381, 388, 387, 389, 300, 390, 382, 391, 345, 409, 410, 392, 393, 411, 412, 301, 414, 394, 415, 413, 303, 416, 400, 417, 347, 419, 420, 401, 418, 421, 429, 422, 430, 424, 348, 436, 425, 426, 437, 423, 351, 349, 427, 395, 443, 428, 444, 350, 450, 451, 396, 352, 397, 402, 398, 403, 399, 404, 431, 405, 407, 432, 433, 406, 434, 435, 408, 438, 439, 440, 445, 441, 457, 446, 442, 447, 458, 452, 448, 453, 449, 454, 455, 459, 456, 460]
+CFG = {"ev":"ssssssss","pev":"svsvsvsvssssssssssss","ew":["vvvv","vvvv","vvvv","vvvv","vvvv","vvvv","vvvv","vvvv"],"cuts":[[[0,4]],[[0,4]],[[0,4]],[[0,4]],[[0,4]],[[0,4]],[[0,2],[2,4]],[[0,1],[1,2],[2,3],[3,4]]],"stores":[[[0,4,1]],[[0,4,1]],[[0,4,1]],[[0,4,1]],[[0,4,1]],[[0,4,1]],[[0,4,1]],[[0,2,1],[2,4,1]]],"nb":[4,6,2,10],"ratio":[2,2,2,2,2,2,2,2,2,2,2,2,2,2],"evs":"ssssssssssssssssssssssssssssssssssssssssssssssssssssssssssssssss","loads":[["a",0],["w",0,[0]],["a",1],["w",1,[0]],["a",2],["w",2,[0]],["w",0,[1]],["w",1,[1]],["w",2,[1]],["c"],["w",0,[2]],["w",1,[2]],["w",2,[2]],["w",0,[3]],["w",1,[3]],["w",2,[3]],["w",0,[4]],["w",1,[4]],["w",2,[4]]],"late":{"0_3":[[0,[5]],[1,[5]],[2,[5]]],"1_3":[[0,[6]],[1,[6]],[2,[6]]],"2_3":[[0,[7]],[1,[7]],[2,[7]]]},"wbufs":{"w0_1":5,"w1_1":5,"w2_1":5},"biasq":"s"}
+ORDER = [0,1,2,5,3,7,6,4,9,8,11,10,13,12,14,15,18,16,19,20,23,25,17,27,21,29,26,31,24,46,30,47,28,48,22,49,33,32,36,34,37,38,41,39,42,35,54,43,55,40,50,44,56,51,52,57,53,45,59,58,60,61,67,62,68,69,77,63,78,70,79,80,81,71,82,83,85,84,72,86,73,74,89,87,90,75,121,88,94,91,95,76,111,92,112,96,116,97,122,93,117,113,131,98,114,132,118,136,119,123,115,124,133,126,125,127,128,134,129,120,144,138,145,130,146,147,102,137,135,163,148,164,168,139,165,149,64,150,166,151,140,152,173,104,170,174,65,175,153,103,176,169,177,154,183,184,167,188,66,178,105,179,171,180,99,106,181,193,185,182,194,195,186,196,100,172,189,190,197,212,213,191,217,187,198,214,101,192,199,200,215,156,201,222,109,223,202,219,224,225,107,216,218,232,155,226,233,220,237,108,227,234,228,221,110,141,229,235,230,157,142,242,243,239,231,244,245,203,238,236,261,246,262,143,266,158,247,240,248,205,249,161,263,250,241,271,272,264,251,273,274,268,267,265,281,159,275,282,269,286,276,160,283,277,270,278,162,279,284,291,280,292,288,293,294,285,287,204,295,310,252,311,315,206,296,207,297,298,289,299,254,210,320,312,321,300,322,316,313,290,330,331,317,314,335,323,318,325,324,326,332,327,328,319,333,340,341,329,337,342,343,336,334,208,359,344,253,360,364,338,209,345,346,361,339,211,347,348,255,362,369,370,349,371,366,372,365,301,363,379,373,380,384,374,256,367,375,303,376,259,377,381,389,368,390,382,391,378,392,385,386,393,394,387,395,383,396,397,257,388,415,416,302,398,417,418,350,420,258,421,422,419,260,423,425,426,351,424,427,428,399,304,430,431,432,429,400,433,406,305,407,434,308,306,352,435,436,307,442,443,353,449,309,450,354,456,457,401,355,357,402,403,356,404,405,358,408,409,410,437,411,413,438,439,412,440,441,414,444,445,446,451,447,463,452,448,453,464,458,454,459,455,460,461,465,462,466]
+EMAP = {"2":"s","3":"v","15":"s","16":"v","20":"s","21":"s","33":"s","34":"s","38":"v","39":"s","43":"s","44":"s","56":"v","57":"s","61":"s","62":"v","69":"s","70":"s","74":"s","75":"s","91":"s","92":"s","96":"v","97":"s","113":"s","114":"s","118":"v","119":"s","133":"s","134":"s","138":"s","139":"v","165":"s","166":"s","170":"s","171":"s","185":"s","186":"s","190":"s","191":"s","214":"s","215":"s","219":"s","220":"s","234":"s","235":"s","239":"s","240":"s","263":"s","264":"s","268":"s","269":"s","283":"s","284":"s","288":"s","289":"s","312":"s","313":"s","317":"s","318":"s","332":"s","333":"s","337":"s","338":"s","361":"s","362":"s","366":"s","367":"s","381":"s","382":"s","386":"s","387":"s"}
 
 
 def tile_structuredlstmcell_kernel(
@@ -40,11 +41,11 @@ def tile_structuredlstmcell_kernel(
     with ExitStack() as ctx:
         ctx.enter_context(tc.manual_schedule())
         const = ctx.enter_context(tc.tile_pool(name="const", bufs=1))
-        rawp = ctx.enter_context(tc.tile_pool(name="rawp", bufs=NB_RAW))
-        gpool = ctx.enter_context(tc.tile_pool(name="gpool", bufs=8))
-        cpool = ctx.enter_context(tc.tile_pool(name="cpool", bufs=8))
-        prep = ctx.enter_context(tc.tile_pool(name="prep", bufs=4))
-        outp = ctx.enter_context(tc.tile_pool(name="outp", bufs=3))
+        rawp = ctx.enter_context(tc.tile_pool(name="rawp", bufs=3))
+        gpool = ctx.enter_context(tc.tile_pool(name="gpool", bufs=CFG["nb"][1]))
+        cpool = ctx.enter_context(tc.tile_pool(name="cpool", bufs=CFG["nb"][3]))
+        prep = ctx.enter_context(tc.tile_pool(name="prep", bufs=CFG["nb"][0]))
+        outp = ctx.enter_context(tc.tile_pool(name="outp", bufs=CFG["nb"][2]))
         psum = ctx.enter_context(tc.psum_pool(name="psum", bufs=1))
 
         ident_f = const.tile([128, 128], F32, name="ident_f")
@@ -54,51 +55,53 @@ def tile_structuredlstmcell_kernel(
         warm = const.tile([128, 1], F32, name="warm")
         nc.vector.memset(warm[:], 0.0)
         for gi in range(4):
-            nc.scalar.dma_start(
+            (nc.gpsimd if CFG["biasq"] == "g" else nc.scalar).dma_start(
                 out=bz[2 * gi:2 * gi + 2, :],
                 in_=biases[gi].rearrange("(r n) -> r n", r=2),
             )
         nc.scalar.activation(out=warm[:], in_=warm[:], func=ACT.Sigmoid)
         ident_b = const.tile([128, 128], BF16, name="ident_b")
         nc.vector.tensor_copy(out=ident_b[:], in_=ident_f[:])
-        bias_sb = const.tile([128, 4, 1024], F32, name="bias_sb")
+        bias_sb = const.tile([128, 4, 1024], BF16, name="bias_sb")
 
-        raw_act = []
-        for s in range(3):
-            raw_act.append(const.tile([128, 4 * k_src[s]], BF16, name="ra%d" % s))
         cell_sb = const.tile([128, 4, 1024], BF16, name="cell_sb")
         acodes = const.tile([128, 4, 512], U32, name="acodes", align_bytes=64)
         ascales = const.tile([128, 4, 512], U8, name="ascales", align_bytes=64)
 
+        raw_act = [None, None, None]
+
         def load_act(s):
+            raw_act[s] = rawp.tile([128, 4 * k_src[s]], BF16, name="ra%d" % s, tag="ra%d" % s, bufs=1)
             nc.sync.dma_start(out=raw_act[s][:], in_=acts[s].rearrange("(p t) k -> p (t k)", t=4))
 
         raw_w = {}
 
-        def load_w(j, s):
+        def load_w(grp_blocks, s):
             k = k_src[s]
-            t = rawp.tile([128, 4 * k], BF16, name="rw%d" % s, tag="rw%d" % s)
+            nb = len(grp_blocks)
+            j0 = grp_blocks[0]
+            tag = "w%d_%d" % (s, nb)
+            t = rawp.tile([128, 4 * nb * k], BF16, name=tag, tag=tag, bufs=CFG["wbufs"][tag])
             for gi in range(4):
-                nc.sync.dma_start(out=t[:, gi * k:(gi + 1) * k], in_=w_src[s][gi][j * 128:(j + 1) * 128, :])
-            raw_w[(j, s)] = t
+                nc.sync.dma_start(
+                    out=t[:, gi * nb * k:(gi + 1) * nb * k].rearrange("p (s k) -> p s k", s=nb),
+                    in_=w_src[s][gi][j0 * 128:(j0 + nb) * 128, :].rearrange("(s p) k -> p s k", p=128),
+                )
+            for i, j in enumerate(grp_blocks):
+                raw_w[(j, s)] = (t, nb, i)
 
         def load_cell():
             nc.sync.dma_start(
                 out=cell_sb[:].rearrange("p t h -> p (t h)"), in_=cell.rearrange("(p t) h -> p (t h)", t=4)
             )
 
-        load_act(0)
-        load_w(0, 0)
-        load_act(1)
-        load_w(0, 1)
-        load_act(2)
-        load_w(0, 2)
-        for s in range(3):
-            load_w(1, s)
-        load_cell()
-        for j in range(2, NB_RAW):
-            for s in range(3):
-                load_w(j, s)
+        for item in CFG["loads"]:
+            if item[0] == "a":
+                load_act(item[1])
+            elif item[0] == "c":
+                load_cell()
+            else:
+                load_w(item[2], item[1])
 
         free_banks = list(range(8))
 
@@ -122,24 +125,21 @@ def tile_structuredlstmcell_kernel(
         out_h = out_0.rearrange("(p t) h -> p t h", t=4)
         out_c = out_1.rearrange("(p t) h -> p t h", t=4)
 
-        def tiles_of(j):
-            if j < 0:
-                return raw_act
-            return [raw_w[(j, 0)], raw_w[(j, 1)], raw_w[(j, 2)]]
-
         def t_bank(j, c, a):
-            tl = tiles_of(j)
-            if c < 2:
-                raw, kw, off = tl[c], 256, 0
+            s = min(c, 2)
+            kw = k_src[s] // 2
+            off = 256 * (c - 2) if c > 2 else 0
+            if j < 0:
+                raw, nb, i = raw_act[s], 1, 0
             else:
-                raw, kw, off = tl[2], 512, 256 * (c - 2)
+                raw, nb, i = raw_w[(j, s)]
             rw = raw[:].bitcast(F32)
             if a == 0:
                 grp_of[(j, c)] = gpool.tile([128, 2048], BF16, name="grp", tag="grp", align_bytes=64)
             b, xt = bank_tile([128, 2, 256])
             for g2 in range(2):
                 for u in range(2):
-                    col = (2 * a + g2) * kw + off + 128 * u
+                    col = ((2 * a + g2) * nb + i) * kw + off + 128 * u
                     nc.tensor.transpose(xt[:, u, g2 * 128:(g2 + 1) * 128], rw[:, col:col + 128], ident_f[:])
             xt_of[(j, c, a)] = (b, xt)
 
@@ -225,31 +225,40 @@ def tile_structuredlstmcell_kernel(
             eng_of[e].tensor_tensor(out=gi, in0=gi, in1=pre_of[j][:, b0:b1, 384:512], op=ALU.mult)
 
         def add_c(e, j, b0, b1):
-            if j not in c_of:
-                c_of[j] = outp.tile([128, 4, 128], F32, name="co", tag="co")
+            if j // 2 not in c_of:
+                c_of[j // 2] = outp.tile([128, 4, 256], F32, name="co", tag="co")
             eng_of[e].tensor_tensor(
-                out=c_of[j][:, b0:b1, :], in0=pre_of[j][:, b0:b1, 128:256], in1=pre_of[j][:, b0:b1, 0:128], op=ALU.add
+                out=c_of[j // 2][:, b0:b1, (j % 2) * 128:(j % 2) * 128 + 128], in0=pre_of[j][:, b0:b1, 128:256], in1=pre_of[j][:, b0:b1, 0:128], op=ALU.add
             )
 
         def tanh_cell(j, b0, b1):
-            nc.scalar.activation(out=pre_of[j][:, b0:b1, 384:512], in_=c_of[j][:, b0:b1, :], func=ACT.Tanh)
+            nc.scalar.activation(out=pre_of[j][:, b0:b1, 384:512], in_=c_of[j // 2][:, b0:b1, (j % 2) * 128:(j % 2) * 128 + 128], func=ACT.Tanh)
 
         def mul_h(e, j, b0, b1):
-            if j not in h_of:
-                h_of[j] = outp.tile([128, 4, 128], F32, name="ho", tag="ho")
+            if j // 2 not in h_of:
+                h_of[j // 2] = outp.tile([128, 4, 256], F32, name="ho", tag="ho")
             eng_of[e].tensor_tensor(
-                out=h_of[j][:, b0:b1, :], in0=pre_of[j][:, b0:b1, 256:384], in1=pre_of[j][:, b0:b1, 384:512], op=ALU.mult
+                out=h_of[j // 2][:, b0:b1, (j % 2) * 128:(j % 2) * 128 + 128], in0=pre_of[j][:, b0:b1, 256:384], in1=pre_of[j][:, b0:b1, 384:512], op=ALU.mult
             )
 
-        def store_c(j, b0, b1):
-            nc.sync.dma_start(out=out_c[:, b0:b1, j * 128:(j + 1) * 128], in_=c_of[j][:, b0:b1, :])
+        def store_c(j, b0, b1, nbl):
+            lo = (j % 2 + 1 - nbl) * 128
+            nc.sync.dma_start(
+                out=out_c[:, b0:b1, (j + 1 - nbl) * 128:(j + 1) * 128], in_=c_of[j // 2][:, b0:b1, lo:lo + nbl * 128]
+            )
 
-        def store_h(j, b0, b1):
-            nc.sync.dma_start(out=out_h[:, b0:b1, j * 128:(j + 1) * 128], in_=h_of[j][:, b0:b1, :])
+        def store_h(j, b0, b1, nbl):
+            lo = (j % 2 + 1 - nbl) * 128
+            nc.sync.dma_start(
+                out=out_h[:, b0:b1, (j + 1 - nbl) * 128:(j + 1) * 128], in_=h_of[j // 2][:, b0:b1, lo:lo + nbl * 128]
+            )
 
-        def load_block(j):
-            for s in range(3):
-                load_w(j, s)
+        def load_late(s, blocks):
+            load_w(blocks, s)
+
+        def late_loads(j, c):
+            for s, blocks in CFG["late"].get("%d_%d" % (j, c), []):
+                task(load_late, s, blocks)
 
         def chunk(j, c, ev):
             task(t_bank, j, c, 0)
@@ -260,8 +269,10 @@ def tile_structuredlstmcell_kernel(
 
         def epilogue(j):
             cuts = CFG["cuts"][j]
-            e = CFG["ew"][j]
-            for b0, b1 in cuts:
+            for k, (b0, b1) in enumerate(cuts):
+                e = CFG["ew"][j]
+                if not isinstance(e, str):
+                    e = e[k]
                 task(sig, j, b0, b1)
                 task(tanh_g, j, b0, b1)
                 task(mul_fc, e[0], j, b0, b1)
@@ -269,9 +280,9 @@ def tile_structuredlstmcell_kernel(
                 task(add_c, e[2], j, b0, b1)
                 task(tanh_cell, j, b0, b1)
                 task(mul_h, e[3], j, b0, b1)
-            for b0, b1 in CFG["stores"][j]:
-                task(store_c, j, b0, b1)
-                task(store_h, j, b0, b1)
+            for b0, b1, nbl in CFG["stores"][j]:
+                task(store_c, j, b0, b1, nbl)
+                task(store_h, j, b0, b1, nbl)
 
         chunk(-1, 0, CFG["pev"][0:2])
         for r in range(4):
@@ -290,9 +301,10 @@ def tile_structuredlstmcell_kernel(
                 task(mx_pass, 0, bt, c)
         chunk(0, 2, CFG["pev"][12:14])
         chunk(0, 3, CFG["pev"][14:16])
-        task(load_block, NB_RAW)
+        late_loads(0, 3)
         chunk(1, 0, CFG["pev"][16:18])
         chunk(1, 1, CFG["pev"][18:20])
+        late_loads(1, 1)
         for c in (2, 3):
             for bt in range(4):
                 task(mx_pass, 0, bt, c)
@@ -300,24 +312,32 @@ def tile_structuredlstmcell_kernel(
             task(bias_add, 0, bt)
         chunk(1, 2, CFG["ev"][4:6])
         chunk(1, 3, CFG["ev"][6:8])
-        task(load_block, NB_RAW + 1)
+        late_loads(1, 3)
         epilogue(0)
-        for p in range(1, N_BLOCKS):
-            nxt = p + 1
-            per = CFG["run"]
-            for part in range(4 // per):
-                if nxt < N_BLOCKS:
-                    for c in range(part * per, (part + 1) * per):
-                        chunk(nxt, c, CFG["ev"][2 * c:2 * c + 2])
-                    if part == 4 // per - 1 and nxt + NB_RAW < N_BLOCKS:
-                        task(load_block, nxt + NB_RAW)
-                for bt in range(part * per, (part + 1) * per):
+        nxt_chunk = 8
+        nxt_quarter = 4
+        for r in CFG["ratio"]:
+            for i in range(2):
+                if nxt_chunk < 4 * N_BLOCKS:
+                    j, c = nxt_chunk // 4, nxt_chunk % 4
+                    chunk(j, c, CFG["evs"][2 * nxt_chunk:2 * nxt_chunk + 2])
+                    late_loads(j, c)
+                    nxt_chunk += 1
+            for i in range(r):
+                if nxt_quarter < 4 * N_BLOCKS:
+                    p, bt = nxt_quarter // 4, nxt_quarter % 4
+                    assert 4 * (p + 1) <= nxt_chunk
                     for c in range(4):
                         task(mx_pass, p, bt, c)
                     task(bias_add, p, bt)
-            epilogue(p)
+                    if bt == 3:
+                        epilogue(p)
+                    nxt_quarter += 1
+        assert nxt_chunk == 4 * N_BLOCKS and nxt_quarter == 4 * N_BLOCKS
 
         order = ORDER if ORDER else list(range(len(tasks)))
         for i in order:
             fn, args = tasks[i]
+            if str(i) in EMAP:
+                args = args[:-1] + (EMAP[str(i)],)
             fn(*args)

@@ -15,9 +15,9 @@ FLOPS = 2 * 512 * 2048 * 4096
 
 NB_RAW = 5
 N_BLOCKS = 8
-CFG = {"ev":"ssssssss","pev":"svsvsvsvssssssssssss","ew":["vvvv","vvvv","vvvv","vvvv","vvvv","vvvv","vvvv","vvvv"],"cuts":[[[0,4]],[[0,4]],[[0,4]],[[0,4]],[[0,4]],[[0,4]],[[0,2],[2,4]],[[0,1],[1,2],[2,3],[3,4]]],"stores":[[[0,4,1]],[[0,4,1]],[[0,4,1]],[[0,4,1]],[[0,4,1]],[[0,4,1]],[[0,4,1]],[[0,2,1],[2,4,1]]],"nb":[4,6,2,10],"ratio":[2,2,2,2,2,2,2,2,2,2,2,2,2,2],"evs":"ssssssssssssssssssssssssssssssssssssssssssssssssssssssssssssssss","loads":[["a",0],["w",0,[0]],["a",1],["w",1,[0]],["a",2],["w",2,[0]],["w",0,[1]],["w",1,[1]],["w",2,[1]],["c"],["w",0,[2]],["w",1,[2]],["w",2,[2]],["w",0,[3]],["w",1,[3]],["w",2,[3]],["w",0,[4]],["w",1,[4]],["w",2,[4]]],"late":{"0_3":[[0,[5]],[1,[5]],[2,[5]]],"1_3":[[0,[6]],[1,[6]],[2,[6]]],"2_3":[[0,[7]],[1,[7]],[2,[7]]]},"wbufs":{"w0_1":5,"w1_1":5,"w2_1":5},"biasq":"s"}
-ORDER = [0,1,2,5,3,7,6,4,9,8,11,10,13,12,14,15,18,16,19,20,23,25,17,27,21,29,26,31,24,46,30,47,28,48,22,49,33,32,36,34,37,38,41,39,42,35,54,43,55,40,50,44,56,51,52,57,53,45,59,58,60,61,67,62,68,69,77,63,78,70,79,80,81,71,82,83,85,84,72,86,73,74,89,87,90,75,121,88,94,91,95,76,111,92,112,96,116,97,122,93,117,113,131,98,114,132,118,136,119,123,115,124,133,126,125,127,128,134,129,120,144,138,145,130,146,147,102,137,135,163,148,164,168,139,165,149,64,150,166,151,140,152,173,104,170,174,65,175,153,103,176,169,177,154,183,184,167,188,66,178,105,179,171,180,99,106,181,193,185,182,194,195,186,196,100,172,189,190,197,212,213,191,217,187,198,214,101,192,199,200,215,156,201,222,109,223,202,219,224,225,107,216,218,232,155,226,233,220,237,108,227,234,228,221,110,141,229,235,230,157,142,242,243,239,231,244,245,203,238,236,261,246,262,143,266,158,247,240,248,205,249,161,263,250,241,271,272,264,251,273,274,268,267,265,281,159,275,282,269,286,276,160,283,277,270,278,162,279,284,291,280,292,288,293,294,285,287,204,295,310,252,311,315,206,296,207,297,298,289,299,254,210,320,312,321,300,322,316,313,290,330,331,317,314,335,323,318,325,324,326,332,327,328,319,333,340,341,329,337,342,343,336,334,208,359,344,253,360,364,338,209,345,346,361,339,211,347,348,255,362,369,370,349,371,366,372,365,301,363,379,373,380,384,374,256,367,375,303,376,259,377,381,389,368,390,382,391,378,392,385,386,393,394,387,395,383,396,397,257,388,415,416,302,398,417,418,350,420,258,421,422,419,260,423,425,426,351,424,427,428,399,304,430,431,432,429,400,433,406,305,407,434,308,306,352,435,436,307,442,443,353,449,309,450,354,456,457,401,355,357,402,403,356,404,405,358,408,409,410,437,411,413,438,439,412,440,441,414,444,445,446,451,447,463,452,448,453,464,458,454,459,455,460,461,465,462,466]
-EMAP = {"2":"s","3":"v","15":"s","16":"v","20":"s","21":"s","33":"s","34":"s","38":"v","39":"s","43":"s","44":"s","56":"v","57":"s","61":"s","62":"v","69":"s","70":"s","74":"s","75":"s","91":"s","92":"s","96":"v","97":"s","113":"s","114":"s","118":"v","119":"s","133":"s","134":"s","138":"s","139":"v","165":"s","166":"s","170":"s","171":"s","185":"s","186":"s","190":"s","191":"s","214":"s","215":"s","219":"s","220":"s","234":"s","235":"s","239":"s","240":"s","263":"s","264":"s","268":"s","269":"s","283":"s","284":"s","288":"s","289":"s","312":"s","313":"s","317":"s","318":"s","332":"s","333":"s","337":"s","338":"s","361":"s","362":"s","366":"s","367":"s","381":"s","382":"s","386":"s","387":"s"}
+CFG = {"ev":"ssssssss","pev":"svsvsvsvssssssssssss","ew":["vvvv","vvvv","vvvv","vvvv","vvvv","vvvv","vvvv","vvvv"],"cuts":[[[0,4]],[[0,4]],[[0,4]],[[0,4]],[[0,4]],[[0,4]],[[0,2],[2,4]],[[0,1],[1,2],[2,3],[3,4]]],"stores":[[],[[0,4,2]],[],[[0,4,2]],[],[[0,4,2]],[[0,4,1]],[[0,2,1],[2,4,1]]],"nb":[4,6,2,10],"ratio":[2,2,2,2,2,2,2,2,2,2,2,2,2,2],"evs":"ssssssssssssssssssssssssssssssssssssssssssssssssssssssssssssssss","loads":[["a",0],["w",0,[0]],["a",1],["w",1,[0]],["a",2],["w",2,[0]],["w",0,[1]],["w",1,[1]],["w",2,[1]],["w",0,[2,3]],["w",1,[2,3]],["w",2,[2]],["c"],["w",2,[3]],["w",0,[4,5]],["w",1,[4,5]],["w",2,[4]]],"late":{"0_3":[[2,[5]]],"1_3":[[2,[6]]],"2_3":[[2,[7]]],"3_1":[[0,[6,7]],[1,[6,7]]]},"wbufs":{"w0_1":2,"w1_1":2,"w0_2":2,"w1_2":2,"w2_1":5},"biasq":"g"}
+ORDER = [0,1,2,5,3,7,6,9,11,8,10,13,14,12,15,18,4,19,16,23,20,25,21,27,29,26,24,31,32,30,28,33,17,34,22,46,35,47,48,49,50,51,52,53,36,37,38,41,39,42,43,54,40,55,44,59,56,45,60,57,65,61,58,66,62,70,75,67,63,76,77,68,78,79,72,69,80,81,83,82,71,84,87,73,88,85,92,89,115,86,90,93,74,105,94,106,91,95,116,110,107,96,117,108,118,112,109,120,121,98,119,122,123,136,124,137,138,139,99,111,140,125,113,126,101,130,127,141,114,128,142,143,144,132,100,167,168,145,131,155,129,146,156,102,160,169,161,133,148,177,178,157,134,182,158,183,170,162,159,172,173,163,171,174,64,175,179,164,187,188,180,176,189,190,184,204,181,185,205,191,209,206,97,210,186,192,207,193,194,211,208,195,214,212,196,215,135,216,103,213,217,224,147,218,225,226,229,104,230,227,219,149,165,220,231,221,228,222,232,234,150,235,197,236,223,237,253,166,238,254,258,233,255,259,239,199,256,240,260,241,257,153,242,261,263,243,264,151,265,262,266,198,273,267,274,244,278,152,279,268,200,154,269,270,201,275,271,283,246,276,284,285,280,272,286,300,281,287,301,305,302,277,306,303,288,282,289,307,304,290,291,308,310,292,311,202,312,309,313,245,320,314,321,293,325,203,326,315,247,316,317,322,248,318,330,323,295,251,331,332,327,319,333,349,328,334,350,351,354,324,355,352,335,329,356,336,353,337,338,357,359,339,360,249,361,358,362,294,369,363,340,370,374,250,375,364,296,252,365,371,366,297,367,372,379,342,380,376,381,368,382,377,384,383,385,298,386,387,373,405,341,406,388,389,407,378,390,299,396,408,410,343,411,397,412,409,413,415,344,425,416,417,426,414,418,347,345,420,421,419,432,422,433,423,346,439,440,424,348,391,446,392,447,393,398,394,399,395,400,427,401,403,428,429,402,430,431,404,434,435,436,441,437,453,442,438,443,454,448,444,449,445,450,451,455,452,456]
+EMAP = {"2":"s","3":"v","15":"s","16":"s","20":"v","21":"s","33":"s","34":"s","38":"s","39":"v","43":"s","44":"s","56":"s","57":"s","61":"s","62":"s","67":"s","68":"s","72":"s","73":"s","89":"s","90":"s","94":"s","95":"s","107":"s","108":"s","112":"s","113":"s","127":"s","128":"s","132":"s","133":"s","157":"s","158":"s","162":"s","163":"s","179":"s","180":"s","184":"s","185":"s","206":"s","207":"s","211":"s","212":"s","226":"s","227":"s","231":"s","232":"s","255":"s","256":"s","260":"s","261":"s","275":"s","276":"s","280":"s","281":"s","302":"s","303":"s","307":"s","308":"s","322":"s","323":"s","327":"s","328":"s","351":"s","352":"s","356":"s","357":"s","371":"s","372":"s","376":"s","377":"s"}
 
 
 def tile_structuredlstmcell_kernel(

@@ -11,333 +11,323 @@ FP8X4 = mybir.dt.float8_e4m3fn_x4
 ACT = mybir.ActivationFunctionType
 ALU = mybir.AluOpType
 
-FLOPS = 2 * 512 * 2048 * 4096
+BATCH = 512
+HIDDEN = 1024
+K_TOTAL = 2048
+FLOPS = 2 * BATCH * K_TOTAL * 4 * HIDDEN
 
-NB_RAW = 5
-N_BLOCKS = 8
-CFG = {"ev":"ssssssss","pev":"svsvsvsvssssssssssss","ew":["vvvv","vvvv","vvvv","vvvv","vvvv","vvvv","vvvv","vvvv"],"cuts":[[[0,4]],[[0,4]],[[0,4]],[[0,4]],[[0,4]],[[0,4]],[[0,2],[2,4]],[[0,1],[1,2],[2,3],[3,4]]],"stores":[[],[[0,4,2]],[],[[0,4,2]],[],[[0,4,2]],[[0,4,1]],[[0,2,1],[2,4,1]]],"nb":[4,6,2,10],"ratio":[2,2,2,2,2,2,2,2,2,2,2,2,2,2],"evs":"ssssssssssssssssssssssssssssssssssssssssssssssssssssssssssssssss","loads":[["a",0],["w",0,[0]],["a",1],["w",1,[0]],["a",2],["w",2,[0]],["w",0,[1]],["w",1,[1]],["w",2,[1]],["w",0,[2,3]],["w",1,[2,3]],["w",2,[2]],["c"],["w",2,[3]],["w",0,[4,5]],["w",1,[4,5]],["w",2,[4]]],"late":{"0_3":[[2,[5]]],"1_3":[[2,[6]]],"2_3":[[2,[7]]],"3_1":[[0,[6,7]],[1,[6,7]]]},"wbufs":{"w0_1":2,"w1_1":2,"w0_2":2,"w1_2":2,"w2_1":5},"biasq":"g"}
-ORDER = [0,1,2,5,3,7,6,9,11,8,10,13,14,12,15,18,4,19,16,23,20,25,21,27,29,26,24,31,32,30,28,33,17,34,22,46,35,47,48,49,50,51,52,53,36,37,38,41,39,42,43,54,40,55,44,59,56,45,60,57,65,61,58,66,62,70,75,67,63,76,77,68,78,79,72,69,80,81,83,82,71,84,87,73,88,85,92,89,115,86,90,93,74,105,94,106,91,95,116,110,107,96,117,108,118,112,109,120,121,98,119,122,123,136,124,137,138,139,99,111,140,125,113,126,101,130,127,141,114,128,142,143,144,132,100,167,168,145,131,155,129,146,156,102,160,169,161,133,148,177,178,157,134,182,158,183,170,162,159,172,173,163,171,174,64,175,179,164,187,188,180,176,189,190,184,204,181,185,205,191,209,206,97,210,186,192,207,193,194,211,208,195,214,212,196,215,135,216,103,213,217,224,147,218,225,226,229,104,230,227,219,149,165,220,231,221,228,222,232,234,150,235,197,236,223,237,253,166,238,254,258,233,255,259,239,199,256,240,260,241,257,153,242,261,263,243,264,151,265,262,266,198,273,267,274,244,278,152,279,268,200,154,269,270,201,275,271,283,246,276,284,285,280,272,286,300,281,287,301,305,302,277,306,303,288,282,289,307,304,290,291,308,310,292,311,202,312,309,313,245,320,314,321,293,325,203,326,315,247,316,317,322,248,318,330,323,295,251,331,332,327,319,333,349,328,334,350,351,354,324,355,352,335,329,356,336,353,337,338,357,359,339,360,249,361,358,362,294,369,363,340,370,374,250,375,364,296,252,365,371,366,297,367,372,379,342,380,376,381,368,382,377,384,383,385,298,386,387,373,405,341,406,388,389,407,378,390,299,396,408,410,343,411,397,412,409,413,415,344,425,416,417,426,414,418,347,345,420,421,419,432,422,433,423,346,439,440,424,348,391,446,392,447,393,398,394,399,395,400,427,401,403,428,429,402,430,431,404,434,435,436,441,437,453,442,438,443,454,448,444,449,445,450,451,455,452,456]
-EMAP = {"2":"s","3":"v","15":"s","16":"s","20":"v","21":"s","33":"s","34":"s","38":"s","39":"v","43":"s","44":"s","56":"s","57":"s","61":"s","62":"s","67":"s","68":"s","72":"s","73":"s","89":"s","90":"s","94":"s","95":"s","107":"s","108":"s","112":"s","113":"s","127":"s","128":"s","132":"s","133":"s","157":"s","158":"s","162":"s","163":"s","179":"s","180":"s","184":"s","185":"s","206":"s","207":"s","211":"s","212":"s","226":"s","227":"s","231":"s","232":"s","255":"s","256":"s","260":"s","261":"s","275":"s","276":"s","280":"s","281":"s","302":"s","303":"s","307":"s","308":"s","322":"s","323":"s","327":"s","328":"s","351":"s","352":"s","356":"s","357":"s","371":"s","372":"s","376":"s","377":"s"}
+P = 128
+N_TILES = BATCH // P
+N_BLOCKS = HIDDEN // P
+N_CHUNKS = 4
+N_GATES = 4
+GATE_COLS = N_GATES * P
+WORDS = 256
+ACTS = -1
+RAW_BLOCKS = 5
 
 
 def tile_structuredlstmcell_kernel(
-    tc, P, hidden, cell, ext_input,
+    tc, p_in, hidden, cell, ext_input,
     W_pi, b_pi, W_pf, b_pf, W_pg, b_pg, W_po, b_po,
     W_hi, W_hf, W_hg, W_ho,
     W_xi, W_xf, W_xg, W_xo,
     out_0, out_1,
 ):
     nc = tc.nc
-    w_src = [
+    weights = [
         [W_pi, W_pf, W_po, W_pg],
         [W_xi, W_xf, W_xo, W_xg],
         [W_hi, W_hf, W_ho, W_hg],
     ]
-    k_src = [512, 512, 1024]
     biases = [b_pi, b_pf, b_po, b_pg]
-    acts = [P, ext_input, hidden]
-    eng_of = {"v": nc.vector, "g": nc.gpsimd}
+    activations = [p_in, ext_input, hidden]
+    k_of = [512, 512, 1024]
+    col_i, col_f, col_o, col_g = [slice(g * P, (g + 1) * P) for g in range(N_GATES)]
 
     with ExitStack() as ctx:
         ctx.enter_context(tc.manual_schedule())
         const = ctx.enter_context(tc.tile_pool(name="const", bufs=1))
-        rawp = ctx.enter_context(tc.tile_pool(name="rawp", bufs=3))
-        gpool = ctx.enter_context(tc.tile_pool(name="gpool", bufs=CFG["nb"][1]))
-        cpool = ctx.enter_context(tc.tile_pool(name="cpool", bufs=CFG["nb"][3]))
-        prep = ctx.enter_context(tc.tile_pool(name="prep", bufs=CFG["nb"][0]))
-        outp = ctx.enter_context(tc.tile_pool(name="outp", bufs=CFG["nb"][2]))
+        raw_pool = ctx.enter_context(tc.tile_pool(name="raw", bufs=RAW_BLOCKS))
+        grouped_pool = ctx.enter_context(tc.tile_pool(name="grouped", bufs=6))
+        code_pool = ctx.enter_context(tc.tile_pool(name="codes", bufs=10))
+        gate_pool = ctx.enter_context(tc.tile_pool(name="gates", bufs=4))
+        out_pool = ctx.enter_context(tc.tile_pool(name="outs", bufs=3))
         psum = ctx.enter_context(tc.psum_pool(name="psum", bufs=1))
 
-        ident_f = const.tile([128, 128], F32, name="ident_f")
-        make_identity(nc, ident_f[:])
-        bz = const.tile([128, 512], BF16, name="bz")
-        nc.vector.memset(bz[:], 0.0)
-        warm = const.tile([128, 1], F32, name="warm")
+        ident_f32 = const.tile([P, P], F32, name="ident_f32")
+        make_identity(nc, ident_f32[:])
+        bias_rows = const.tile([P, GATE_COLS], BF16, name="bias_rows")
+        nc.vector.memset(bias_rows[:], 0.0)
+        warm = const.tile([P, 1], F32, name="warm")
         nc.vector.memset(warm[:], 0.0)
-        for gi in range(4):
-            (nc.gpsimd if CFG["biasq"] == "g" else nc.scalar).dma_start(
-                out=bz[2 * gi:2 * gi + 2, :],
-                in_=biases[gi].rearrange("(r n) -> r n", r=2),
+        for g in range(N_GATES):
+            nc.scalar.dma_start(
+                out=bias_rows[2 * g:2 * g + 2, :], in_=biases[g].rearrange("(r n) -> r n", r=2)
             )
         nc.scalar.activation(out=warm[:], in_=warm[:], func=ACT.Sigmoid)
-        ident_b = const.tile([128, 128], BF16, name="ident_b")
-        nc.vector.tensor_copy(out=ident_b[:], in_=ident_f[:])
-        bias_sb = const.tile([128, 4, 1024], BF16, name="bias_sb")
+        ident_bf16 = const.tile([P, P], BF16, name="ident_bf16")
+        nc.vector.tensor_copy(out=ident_bf16[:], in_=ident_f32[:])
+        bias_all = const.tile([P, N_GATES, HIDDEN], BF16, name="bias_all")
+        cell_sb = const.tile([P, N_TILES, HIDDEN], BF16, name="cell_sb")
+        act_codes = const.tile([P, N_CHUNKS, BATCH], U32, name="act_codes", align_bytes=64)
+        act_scales = const.tile([P, N_CHUNKS, BATCH], U8, name="act_scales", align_bytes=64)
 
-        cell_sb = const.tile([128, 4, 1024], BF16, name="cell_sb")
-        acodes = const.tile([128, 4, 512], U32, name="acodes", align_bytes=64)
-        ascales = const.tile([128, 4, 512], U8, name="ascales", align_bytes=64)
+        raw = {}
 
-        raw_act = [None, None, None]
+        def load_activation(s):
+            raw[(ACTS, s)] = const.tile([P, N_TILES * k_of[s]], BF16, name="raw_act%d" % s)
+            nc.sync.dma_start(out=raw[(ACTS, s)][:], in_=activations[s].rearrange("(p t) k -> p (t k)", t=N_TILES))
 
-        def load_act(s):
-            raw_act[s] = rawp.tile([128, 4 * k_src[s]], BF16, name="ra%d" % s, tag="ra%d" % s, bufs=1)
-            nc.sync.dma_start(out=raw_act[s][:], in_=acts[s].rearrange("(p t) k -> p (t k)", t=4))
+        def load_weights(j, s):
+            k = k_of[s]
+            raw[(j, s)] = raw_pool.tile([P, N_GATES * k], BF16, name="raw_w%d" % s, tag="raw_w%d" % s)
+            for g in range(N_GATES):
+                nc.sync.dma_start(out=raw[(j, s)][:, g * k:(g + 1) * k], in_=weights[s][g][j * P:(j + 1) * P, :])
 
-        raw_w = {}
+        def load_block(j):
+            for s in range(3):
+                load_weights(j, s)
 
-        def load_w(grp_blocks, s):
-            k = k_src[s]
-            nb = len(grp_blocks)
-            j0 = grp_blocks[0]
-            tag = "w%d_%d" % (s, nb)
-            t = rawp.tile([128, 4 * nb * k], BF16, name=tag, tag=tag, bufs=CFG["wbufs"][tag])
-            for gi in range(4):
-                nc.sync.dma_start(
-                    out=t[:, gi * nb * k:(gi + 1) * nb * k].rearrange("p (s k) -> p s k", s=nb),
-                    in_=w_src[s][gi][j0 * 128:(j0 + nb) * 128, :].rearrange("(s p) k -> p s k", p=128),
-                )
-            for i, j in enumerate(grp_blocks):
-                raw_w[(j, s)] = (t, nb, i)
-
-        def load_cell():
-            nc.sync.dma_start(
-                out=cell_sb[:].rearrange("p t h -> p (t h)"), in_=cell.rearrange("(p t) h -> p (t h)", t=4)
-            )
-
-        for item in CFG["loads"]:
-            if item[0] == "a":
-                load_act(item[1])
-            elif item[0] == "c":
-                load_cell()
-            else:
-                load_w(item[2], item[1])
+        for s in range(3):
+            load_activation(s)
+            load_weights(0, s)
+        load_block(1)
+        nc.sync.dma_start(
+            out=cell_sb[:].rearrange("p t h -> p (t h)"), in_=cell.rearrange("(p t) h -> p (t h)", t=N_TILES)
+        )
+        for j in range(2, RAW_BLOCKS):
+            load_block(j)
 
         free_banks = list(range(8))
 
-        def bank_tile(shape):
+        def take_bank(shape):
             b = free_banks.pop(0)
-            t = psum.tile(shape, F32, name="bk%d" % b, tag="bk%d" % b)
-            return b, t
+            return b, psum.tile(shape, F32, name="bank%d" % b, tag="bank%d" % b)
 
-        tasks = []
-
-        def task(fn, *args):
-            tasks.append((fn, args))
-
-        grp_of = {}
-        xt_of = {}
-        q_of = {}
+        grouped = {}
+        w_codes = {}
         acc = {}
-        pre_of = {}
-        c_of = {}
-        h_of = {}
-        out_h = out_0.rearrange("(p t) h -> p t h", t=4)
-        out_c = out_1.rearrange("(p t) h -> p t h", t=4)
+        gates = {}
+        c_new = {}
+        h_new = {}
 
-        def t_bank(j, c, a):
+        def transpose_chunk(j, c, engines):
             s = min(c, 2)
-            kw = k_src[s] // 2
-            off = 256 * (c - 2) if c > 2 else 0
-            if j < 0:
-                raw, nb, i = raw_act[s], 1, 0
-            else:
-                raw, nb, i = raw_w[(j, s)]
-            rw = raw[:].bitcast(F32)
-            if a == 0:
-                grp_of[(j, c)] = gpool.tile([128, 2048], BF16, name="grp", tag="grp", align_bytes=64)
-            b, xt = bank_tile([128, 2, 256])
-            for g2 in range(2):
-                for u in range(2):
-                    col = ((2 * a + g2) * nb + i) * kw + off + 128 * u
-                    nc.tensor.transpose(xt[:, u, g2 * 128:(g2 + 1) * 128], rw[:, col:col + 128], ident_f[:])
-            xt_of[(j, c, a)] = (b, xt)
+            first_word = WORDS * (c - 2) if c > 2 else 0
+            words = raw[(j, s)][:].bitcast(F32)
+            out_tile = grouped_pool.tile([P, 4 * GATE_COLS], BF16, name="grouped", tag="grouped", align_bytes=64)
+            grouped[(j, c)] = out_tile
+            out_words = out_tile[:].bitcast(F32)
+            banks = []
+            for half in range(2):
+                b, bank = take_bank([P, 2, 2 * P])
+                for r in range(2):
+                    for u in range(2):
+                        col = (2 * half + r) * (k_of[s] // 2) + first_word + P * u
+                        nc.tensor.transpose(bank[:, u, r * P:(r + 1) * P], words[:, col:col + P], ident_f32[:])
+                banks.append((b, bank))
+            for half in range(2):
+                b, bank = banks[half]
+                dst = out_words[:, half * GATE_COLS:(half + 1) * GATE_COLS].rearrange("p (n u) -> p n u", u=2)
+                src = bank[:].rearrange("p u n -> p n u")
+                if engines[half] == "s":
+                    nc.scalar.copy(out=dst, in_=src)
+                else:
+                    nc.vector.tensor_copy(out=dst, in_=src)
+                free_banks.append(b)
 
-        def e_bank(j, c, a, e):
-            b, xt = xt_of[(j, c, a)]
-            gw = grp_of[(j, c)][:].bitcast(F32)
-            dst = gw[:, a * 512:(a + 1) * 512].rearrange("p (n u) -> p n u", u=2)
-            src = xt[:].rearrange("p u n -> p n u")
-            if e == "s":
-                nc.scalar.copy(out=dst, in_=src)
+        def quantise(j, c):
+            if j == ACTS:
+                codes, scales = act_codes[:, c, :], act_scales[:, c, :]
             else:
-                nc.vector.tensor_copy(out=dst, in_=src)
-            free_banks.append(b)
+                codes_tile = code_pool.tile([P, GATE_COLS], U32, name="w_codes", tag="w_codes", align_bytes=64)
+                scales_tile = code_pool.tile([P, GATE_COLS], U8, name="w_scales", tag="w_scales", align_bytes=64)
+                w_codes[(j, c)] = (codes_tile, scales_tile)
+                codes, scales = codes_tile[:], scales_tile[:]
+            nc.vector.quantize_mx(out=codes.bitcast(FP8X4), scales=scales, in_=grouped[(j, c)][:])
 
-        def quant(j, c):
-            grp = grp_of[(j, c)]
-            if j < 0:
-                nc.vector.quantize_mx(out=acodes[:, c, :].bitcast(FP8X4), scales=ascales[:, c, :], in_=grp[:])
-            else:
-                wc = cpool.tile([128, 512], U32, name="wc", tag="wc", align_bytes=64)
-                ws = cpool.tile([128, 512], U8, name="ws", tag="ws", align_bytes=64)
-                nc.vector.quantize_mx(out=wc[:].bitcast(FP8X4), scales=ws[:], in_=grp[:])
-                q_of[(j, c)] = (wc, ws)
-
-        def mx_pass(j, bt, c):
+        def mx_pass(j, t, c):
             if c == 0:
-                acc[(j, bt)] = bank_tile([128, 512])
-            wc, ws = q_of[(j, c)]
+                acc[(j, t)] = take_bank([P, GATE_COLS])
+            codes_tile, scales_tile = w_codes[(j, c)]
+            rows = slice(t * P, (t + 1) * P)
             nc.tensor.matmul_mx(
-                out=acc[(j, bt)][1][:],
-                lhsT=acodes[:, c, bt * 128:(bt + 1) * 128].bitcast(FP8X4),
-                lhsT_scale=ascales[:, c, bt * 128:(bt + 1) * 128],
-                rhs=wc[:].bitcast(FP8X4),
-                rhs_scale=ws[:],
+                out=acc[(j, t)][1][:],
+                lhsT=act_codes[:, c, rows].bitcast(FP8X4),
+                lhsT_scale=act_scales[:, c, rows],
+                rhs=codes_tile[:].bitcast(FP8X4),
+                rhs_scale=scales_tile[:],
                 start=(c == 0),
-                stop=(c == 3),
+                stop=(c == N_CHUNKS - 1),
             )
 
-        bias_bank = {}
+        def spread_bias(first_row):
+            for r in range(first_row, first_row + 4):
+                b, bank = take_bank([P, GATE_COLS])
+                nc.tensor.matmul(
+                    out=bank[:], lhsT=ident_bf16[:, r:r + 1].to_broadcast([P, P]), rhs=bias_rows[:], start=True, stop=True
+                )
+                dst = bias_all[:, r // 2, (r % 2) * GATE_COLS:(r % 2 + 1) * GATE_COLS]
+                if r % 2 == 0:
+                    nc.scalar.copy(out=dst, in_=bank[:])
+                else:
+                    nc.vector.tensor_copy(out=dst, in_=bank[:])
+                free_banks.append(b)
 
-        def bias_mm(r):
-            b, t = bank_tile([128, 512])
-            nc.tensor.matmul(
-                out=t[:], lhsT=ident_b[:, r:r + 1].to_broadcast([128, 128]), rhs=bz[:], start=True, stop=True
-            )
-            bias_bank[r] = (b, t)
-
-        def bias_ev(r):
-            b, t = bias_bank[r]
-            dst = bias_sb[:, r // 2, (r % 2) * 512:(r % 2) * 512 + 512]
-            if r % 2 == 0:
-                nc.scalar.copy(out=dst, in_=t[:])
-            else:
-                nc.vector.tensor_copy(out=dst, in_=t[:])
-            free_banks.append(b)
-
-        def bias_add(j, bt):
-            if bt == 0:
-                pre_of[j] = prep.tile([128, 4, 512], F32, name="pre", tag="pre")
-            b, t = acc[(j, bt)]
+        def add_bias(j, t):
+            if t == 0:
+                gates[j] = gate_pool.tile([P, N_TILES, GATE_COLS], F32, name="gates", tag="gates")
+            b, bank = acc[(j, t)]
             nc.vector.tensor_tensor(
-                out=pre_of[j][:, bt, :].rearrange("p (g c) -> p g c", g=4),
-                in0=t[:].rearrange("p (g c) -> p g c", g=4),
-                in1=bias_sb[:, :, j * 128:(j + 1) * 128],
+                out=gates[j][:, t, :].rearrange("p (g c) -> p g c", g=N_GATES),
+                in0=bank[:].rearrange("p (g c) -> p g c", g=N_GATES),
+                in1=bias_all[:, :, j * P:(j + 1) * P],
                 op=ALU.add,
             )
             free_banks.append(b)
 
-        def sig(j, b0, b1):
-            pre = pre_of[j]
-            nc.scalar.activation(out=pre[:, b0:b1, 0:384], in_=pre[:, b0:b1, 0:384], func=ACT.Sigmoid)
+        def passes_and_bias(j, t):
+            for c in range(N_CHUNKS):
+                mx_pass(j, t, c)
+            add_bias(j, t)
 
-        def tanh_g(j, b0, b1):
-            pre = pre_of[j]
-            nc.scalar.activation(out=pre[:, b0:b1, 384:512], in_=pre[:, b0:b1, 384:512], func=ACT.Tanh)
+        def sigmoids(j, t0, t1):
+            v = gates[j][:, t0:t1, 0:3 * P]
+            nc.scalar.activation(out=v, in_=v, func=ACT.Sigmoid)
 
-        def mul_fc(e, j, b0, b1):
-            gf = pre_of[j][:, b0:b1, 128:256]
-            eng_of[e].tensor_tensor(out=gf, in0=gf, in1=cell_sb[:, b0:b1, j * 128:(j + 1) * 128], op=ALU.mult)
+        def tanh_candidate(j, t0, t1):
+            v = gates[j][:, t0:t1, col_g]
+            nc.scalar.activation(out=v, in_=v, func=ACT.Tanh)
 
-        def mul_ig(e, j, b0, b1):
-            gi = pre_of[j][:, b0:b1, 0:128]
-            eng_of[e].tensor_tensor(out=gi, in0=gi, in1=pre_of[j][:, b0:b1, 384:512], op=ALU.mult)
+        def forget_times_cell(j, t0, t1):
+            v = gates[j][:, t0:t1, col_f]
+            nc.vector.tensor_tensor(out=v, in0=v, in1=cell_sb[:, t0:t1, j * P:(j + 1) * P], op=ALU.mult)
 
-        def add_c(e, j, b0, b1):
-            if j // 2 not in c_of:
-                c_of[j // 2] = outp.tile([128, 4, 256], F32, name="co", tag="co")
-            eng_of[e].tensor_tensor(
-                out=c_of[j // 2][:, b0:b1, (j % 2) * 128:(j % 2) * 128 + 128], in0=pre_of[j][:, b0:b1, 128:256], in1=pre_of[j][:, b0:b1, 0:128], op=ALU.add
+        def input_times_candidate(j, t0, t1):
+            v = gates[j][:, t0:t1, col_i]
+            nc.vector.tensor_tensor(out=v, in0=v, in1=gates[j][:, t0:t1, col_g], op=ALU.mult)
+
+        def sum_to_cell(j, t0, t1):
+            if j not in c_new:
+                c_new[j] = out_pool.tile([P, N_TILES, P], F32, name="c_new", tag="c_new")
+            nc.vector.tensor_tensor(
+                out=c_new[j][:, t0:t1, :], in0=gates[j][:, t0:t1, col_f], in1=gates[j][:, t0:t1, col_i], op=ALU.add
             )
 
-        def tanh_cell(j, b0, b1):
-            nc.scalar.activation(out=pre_of[j][:, b0:b1, 384:512], in_=c_of[j // 2][:, b0:b1, (j % 2) * 128:(j % 2) * 128 + 128], func=ACT.Tanh)
+        def tanh_cell(j, t0, t1):
+            nc.scalar.activation(out=gates[j][:, t0:t1, col_g], in_=c_new[j][:, t0:t1, :], func=ACT.Tanh)
 
-        def mul_h(e, j, b0, b1):
-            if j // 2 not in h_of:
-                h_of[j // 2] = outp.tile([128, 4, 256], F32, name="ho", tag="ho")
-            eng_of[e].tensor_tensor(
-                out=h_of[j // 2][:, b0:b1, (j % 2) * 128:(j % 2) * 128 + 128], in0=pre_of[j][:, b0:b1, 256:384], in1=pre_of[j][:, b0:b1, 384:512], op=ALU.mult
+        def output_times_tanh(j, t0, t1):
+            if j not in h_new:
+                h_new[j] = out_pool.tile([P, N_TILES, P], F32, name="h_new", tag="h_new")
+            nc.vector.tensor_tensor(
+                out=h_new[j][:, t0:t1, :], in0=gates[j][:, t0:t1, col_o], in1=gates[j][:, t0:t1, col_g], op=ALU.mult
             )
 
-        def store_c(j, b0, b1, nbl):
-            lo = (j % 2 + 1 - nbl) * 128
-            nc.sync.dma_start(
-                out=out_c[:, b0:b1, (j + 1 - nbl) * 128:(j + 1) * 128], in_=c_of[j // 2][:, b0:b1, lo:lo + nbl * 128]
-            )
+        h_dram = out_0.rearrange("(p t) h -> p t h", t=N_TILES)
+        c_dram = out_1.rearrange("(p t) h -> p t h", t=N_TILES)
 
-        def store_h(j, b0, b1, nbl):
-            lo = (j % 2 + 1 - nbl) * 128
-            nc.sync.dma_start(
-                out=out_h[:, b0:b1, (j + 1 - nbl) * 128:(j + 1) * 128], in_=h_of[j // 2][:, b0:b1, lo:lo + nbl * 128]
-            )
+        def store(dram, tiles, j, t0, t1):
+            nc.sync.dma_start(out=dram[:, t0:t1, j * P:(j + 1) * P], in_=tiles[j][:, t0:t1, :])
 
-        def load_late(s, blocks):
-            load_w(blocks, s)
-
-        def late_loads(j, c):
-            for s, blocks in CFG["late"].get("%d_%d" % (j, c), []):
-                task(load_late, s, blocks)
-
-        def chunk(j, c, ev):
-            task(t_bank, j, c, 0)
-            task(t_bank, j, c, 1)
-            task(e_bank, j, c, 0, ev[0])
-            task(e_bank, j, c, 1, ev[1])
-            task(quant, j, c)
-
-        def epilogue(j):
-            cuts = CFG["cuts"][j]
-            for k, (b0, b1) in enumerate(cuts):
-                e = CFG["ew"][j]
-                if not isinstance(e, str):
-                    e = e[k]
-                task(sig, j, b0, b1)
-                task(tanh_g, j, b0, b1)
-                task(mul_fc, e[0], j, b0, b1)
-                task(mul_ig, e[1], j, b0, b1)
-                task(add_c, e[2], j, b0, b1)
-                task(tanh_cell, j, b0, b1)
-                task(mul_h, e[3], j, b0, b1)
-            for b0, b1, nbl in CFG["stores"][j]:
-                task(store_c, j, b0, b1, nbl)
-                task(store_h, j, b0, b1, nbl)
-
-        chunk(-1, 0, CFG["pev"][0:2])
-        for r in range(4):
-            task(bias_mm, r)
-            task(bias_ev, r)
-        chunk(0, 0, CFG["pev"][2:4])
-        chunk(-1, 1, CFG["pev"][4:6])
-        for r in range(4, 8):
-            task(bias_mm, r)
-            task(bias_ev, r)
-        chunk(0, 1, CFG["pev"][6:8])
-        chunk(-1, 2, CFG["pev"][8:10])
-        chunk(-1, 3, CFG["pev"][10:12])
+        transpose_chunk(ACTS, 0, "sv")
+        spread_bias(0)
+        transpose_chunk(0, 0, "sv")
+        quantise(ACTS, 0)
+        transpose_chunk(ACTS, 1, "sv")
+        quantise(0, 0)
+        spread_bias(4)
+        transpose_chunk(0, 1, "sv")
+        quantise(ACTS, 1)
+        transpose_chunk(ACTS, 2, "ss")
+        quantise(0, 1)
+        transpose_chunk(ACTS, 3, "ss")
         for c in (0, 1):
-            for bt in range(4):
-                task(mx_pass, 0, bt, c)
-        chunk(0, 2, CFG["pev"][12:14])
-        chunk(0, 3, CFG["pev"][14:16])
-        late_loads(0, 3)
-        chunk(1, 0, CFG["pev"][16:18])
-        chunk(1, 1, CFG["pev"][18:20])
-        late_loads(1, 1)
+            for t in range(N_TILES):
+                mx_pass(0, t, c)
+        quantise(ACTS, 2)
+        quantise(ACTS, 3)
+        transpose_chunk(0, 2, "ss")
+        transpose_chunk(0, 3, "ss")
+        load_block(RAW_BLOCKS)
+        quantise(0, 2)
+        quantise(0, 3)
+        transpose_chunk(1, 0, "ss")
+        transpose_chunk(1, 1, "ss")
         for c in (2, 3):
-            for bt in range(4):
-                task(mx_pass, 0, bt, c)
-        for bt in range(4):
-            task(bias_add, 0, bt)
-        chunk(1, 2, CFG["ev"][4:6])
-        chunk(1, 3, CFG["ev"][6:8])
-        late_loads(1, 3)
-        epilogue(0)
-        nxt_chunk = 8
-        nxt_quarter = 4
-        for r in CFG["ratio"]:
-            for i in range(2):
-                if nxt_chunk < 4 * N_BLOCKS:
-                    j, c = nxt_chunk // 4, nxt_chunk % 4
-                    chunk(j, c, CFG["evs"][2 * nxt_chunk:2 * nxt_chunk + 2])
-                    late_loads(j, c)
-                    nxt_chunk += 1
-            for i in range(r):
-                if nxt_quarter < 4 * N_BLOCKS:
-                    p, bt = nxt_quarter // 4, nxt_quarter % 4
-                    assert 4 * (p + 1) <= nxt_chunk
-                    for c in range(4):
-                        task(mx_pass, p, bt, c)
-                    task(bias_add, p, bt)
-                    if bt == 3:
-                        epilogue(p)
-                    nxt_quarter += 1
-        assert nxt_chunk == 4 * N_BLOCKS and nxt_quarter == 4 * N_BLOCKS
+            for t in range(N_TILES):
+                mx_pass(0, t, c)
+        quantise(1, 0)
+        quantise(1, 1)
+        for t in range(N_TILES):
+            add_bias(0, t)
+        transpose_chunk(1, 2, "ss")
+        transpose_chunk(1, 3, "ss")
+        load_block(RAW_BLOCKS + 1)
+        quantise(1, 2)
+        quantise(1, 3)
 
-        order = ORDER if ORDER else list(range(len(tasks)))
-        for i in order:
-            fn, args = tasks[i]
-            if str(i) in EMAP:
-                args = args[:-1] + (EMAP[str(i)],)
-            fn(*args)
+        for j in range(1, N_BLOCKS - 1):
+            transpose_chunk(j + 1, 0, "ss")
+            transpose_chunk(j + 1, 1, "ss")
+            quantise(j + 1, 0)
+            quantise(j + 1, 1)
+            sigmoids(j - 1, 0, N_TILES)
+            tanh_candidate(j - 1, 0, N_TILES)
+            passes_and_bias(j, 0)
+            passes_and_bias(j, 1)
+            forget_times_cell(j - 1, 0, N_TILES)
+            input_times_candidate(j - 1, 0, N_TILES)
+            sum_to_cell(j - 1, 0, N_TILES)
+            store(c_dram, c_new, j - 1, 0, N_TILES)
+            transpose_chunk(j + 1, 2, "ss")
+            transpose_chunk(j + 1, 3, "ss")
+            if j + 1 + RAW_BLOCKS < N_BLOCKS:
+                load_block(j + 1 + RAW_BLOCKS)
+            tanh_cell(j - 1, 0, N_TILES)
+            quantise(j + 1, 2)
+            quantise(j + 1, 3)
+            passes_and_bias(j, 2)
+            output_times_tanh(j - 1, 0, N_TILES)
+            store(h_dram, h_new, j - 1, 0, N_TILES)
+            passes_and_bias(j, 3)
+
+        last = N_BLOCKS - 1
+        prev = last - 1
+        sigmoids(prev, 0, 2)
+        tanh_candidate(prev, 0, 2)
+        sigmoids(prev, 2, 4)
+        tanh_candidate(prev, 2, 4)
+        forget_times_cell(prev, 0, 2)
+        passes_and_bias(last, 0)
+        input_times_candidate(prev, 0, 2)
+        passes_and_bias(last, 1)
+        sum_to_cell(prev, 0, 2)
+        forget_times_cell(prev, 2, 4)
+        sigmoids(last, 0, 2)
+        tanh_cell(prev, 0, 2)
+        tanh_candidate(last, 0, 2)
+        passes_and_bias(last, 2)
+        output_times_tanh(prev, 0, 2)
+        passes_and_bias(last, 3)
+        input_times_candidate(prev, 2, 4)
+        sum_to_cell(prev, 2, 4)
+        store(c_dram, c_new, prev, 0, N_TILES)
+        sigmoids(last, 2, 4)
+        tanh_cell(prev, 2, 4)
+        tanh_candidate(last, 2, 4)
+        for t0 in (0, 2):
+            forget_times_cell(last, t0, t0 + 2)
+            input_times_candidate(last, t0, t0 + 2)
+            if t0 == 0:
+                output_times_tanh(prev, 2, 4)
+                store(h_dram, h_new, prev, 0, N_TILES)
+            else:
+                output_times_tanh(last, 0, 2)
+                store(h_dram, h_new, last, 0, 2)
+            sum_to_cell(last, t0, t0 + 2)
+            store(c_dram, c_new, last, t0, t0 + 2)
+            tanh_cell(last, t0, t0 + 2)
+        output_times_tanh(last, 2, 4)
+        store(h_dram, h_new, last, 2, 4)

@@ -187,9 +187,12 @@ def tile_structuredlstmcell_kernel(
             )
             free_banks.append(b)
 
-        def passes_and_bias(j, t):
+        def passes(j, t):
             for c in range(N_CHUNKS):
                 mx_pass(j, t, c)
+
+        def passes_and_bias(j, t):
+            passes(j, t)
             add_bias(j, t)
 
         def sigmoids(j, t0, t1):
@@ -270,25 +273,27 @@ def tile_structuredlstmcell_kernel(
 
         for j in range(1, N_BLOCKS - 1):
             transpose_chunk(j + 1, 0, "ss")
+            passes(j, 0)
             transpose_chunk(j + 1, 1, "ss")
             quantise(j + 1, 0)
             quantise(j + 1, 1)
             sigmoids(j - 1, 0, N_TILES)
             tanh_candidate(j - 1, 0, N_TILES)
-            passes_and_bias(j, 0)
+            add_bias(j, 0)
             passes_and_bias(j, 1)
             forget_times_cell(j - 1, 0, N_TILES)
             input_times_candidate(j - 1, 0, N_TILES)
             sum_to_cell(j - 1, 0, N_TILES)
             store(c_dram, c_new, j - 1, 0, N_TILES)
             transpose_chunk(j + 1, 2, "ss")
+            passes(j, 2)
             transpose_chunk(j + 1, 3, "ss")
             if j + 1 + RAW_BLOCKS < N_BLOCKS:
                 load_block(j + 1 + RAW_BLOCKS)
             tanh_cell(j - 1, 0, N_TILES)
             quantise(j + 1, 2)
             quantise(j + 1, 3)
-            passes_and_bias(j, 2)
+            add_bias(j, 2)
             output_times_tanh(j - 1, 0, N_TILES)
             store(h_dram, h_new, j - 1, 0, N_TILES)
             passes_and_bias(j, 3)

@@ -22,7 +22,7 @@ N_BLOCKS = HIDDEN // P
 N_CHUNKS = 4
 N_GATES = 4
 GATE_COLS = N_GATES * P
-WORDS = 256
+CHUNK_WORDS = 256
 ACTS = -1
 RAW_BLOCKS = 5
 
@@ -77,7 +77,11 @@ def tile_structuredlstmcell_kernel(
 
         def load_activation(s):
             raw[(ACTS, s)] = const.tile([P, N_TILES * k_of[s]], BF16, name="raw_act%d" % s)
-            nc.sync.dma_start(out=raw[(ACTS, s)][:], in_=activations[s].rearrange("(p t) k -> p (t k)", t=N_TILES))
+            view = activations[s].rearrange("(p t) k -> p (t k)", t=N_TILES)
+            half_cols = 2 * k_of[s]
+            for part in range(2):
+                cols = slice(part * half_cols, (part + 1) * half_cols)
+                nc.sync.dma_start(out=raw[(ACTS, s)][:, cols], in_=view[:, cols])
 
         def load_weights(j, s):
             k = k_of[s]
@@ -114,7 +118,7 @@ def tile_structuredlstmcell_kernel(
 
         def transpose_chunk(j, c, engines):
             s = min(c, 2)
-            first_word = WORDS * (c - 2) if c > 2 else 0
+            first_word = CHUNK_WORDS * (c - 2) if c > 2 else 0
             words = raw[(j, s)][:].bitcast(F32)
             out_tile = grouped_pool.tile([P, 4 * GATE_COLS], BF16, name="grouped", tag="grouped", align_bytes=64)
             grouped[(j, c)] = out_tile
@@ -122,10 +126,10 @@ def tile_structuredlstmcell_kernel(
             banks = []
             for half in range(2):
                 b, bank = take_bank([P, 2, 2 * P])
-                for r in range(2):
+                for rg in range(2):
                     for u in range(2):
-                        col = (2 * half + r) * (k_of[s] // 2) + first_word + P * u
-                        nc.tensor.transpose(bank[:, u, r * P:(r + 1) * P], words[:, col:col + P], ident_f32[:])
+                        col = (2 * half + rg) * (k_of[s] // 2) + first_word + P * u
+                        nc.tensor.transpose(bank[:, u, rg * P:(rg + 1) * P], words[:, col:col + P], ident_f32[:])
                 banks.append((b, bank))
             for half in range(2):
                 b, bank = banks[half]
@@ -180,19 +184,16 @@ def tile_structuredlstmcell_kernel(
                 gates[j] = gate_pool.tile([P, N_TILES, GATE_COLS], F32, name="gates", tag="gates")
             b, bank = acc[(j, t)]
             nc.vector.tensor_tensor(
-                out=gates[j][:, t, :].rearrange("p (g c) -> p g c", g=N_GATES),
-                in0=bank[:].rearrange("p (g c) -> p g c", g=N_GATES),
+                out=gates[j][:, t, :].rearrange("p (g n) -> p g n", g=N_GATES),
+                in0=bank[:].rearrange("p (g n) -> p g n", g=N_GATES),
                 in1=bias_all[:, :, j * P:(j + 1) * P],
                 op=ALU.add,
             )
             free_banks.append(b)
 
-        def passes(j, t):
+        def passes_and_bias(j, t):
             for c in range(N_CHUNKS):
                 mx_pass(j, t, c)
-
-        def passes_and_bias(j, t):
-            passes(j, t)
             add_bias(j, t)
 
         def sigmoids(j, t0, t1):
@@ -273,27 +274,25 @@ def tile_structuredlstmcell_kernel(
 
         for j in range(1, N_BLOCKS - 1):
             transpose_chunk(j + 1, 0, "ss")
-            passes(j, 0)
             transpose_chunk(j + 1, 1, "ss")
             quantise(j + 1, 0)
             quantise(j + 1, 1)
             sigmoids(j - 1, 0, N_TILES)
             tanh_candidate(j - 1, 0, N_TILES)
-            add_bias(j, 0)
+            passes_and_bias(j, 0)
             passes_and_bias(j, 1)
             forget_times_cell(j - 1, 0, N_TILES)
             input_times_candidate(j - 1, 0, N_TILES)
             sum_to_cell(j - 1, 0, N_TILES)
             store(c_dram, c_new, j - 1, 0, N_TILES)
             transpose_chunk(j + 1, 2, "ss")
-            passes(j, 2)
             transpose_chunk(j + 1, 3, "ss")
             if j + 1 + RAW_BLOCKS < N_BLOCKS:
                 load_block(j + 1 + RAW_BLOCKS)
             tanh_cell(j - 1, 0, N_TILES)
             quantise(j + 1, 2)
             quantise(j + 1, 3)
-            add_bias(j, 2)
+            passes_and_bias(j, 2)
             output_times_tanh(j - 1, 0, N_TILES)
             store(h_dram, h_new, j - 1, 0, N_TILES)
             passes_and_bias(j, 3)
@@ -322,17 +321,19 @@ def tile_structuredlstmcell_kernel(
         sigmoids(last, 2, 4)
         tanh_cell(prev, 2, 4)
         tanh_candidate(last, 2, 4)
-        for t0 in (0, 2):
-            forget_times_cell(last, t0, t0 + 2)
-            input_times_candidate(last, t0, t0 + 2)
-            if t0 == 0:
-                output_times_tanh(prev, 2, 4)
-                store(h_dram, h_new, prev, 0, N_TILES)
-            else:
-                output_times_tanh(last, 0, 2)
-                store(h_dram, h_new, last, 0, 2)
-            sum_to_cell(last, t0, t0 + 2)
-            store(c_dram, c_new, last, t0, t0 + 2)
-            tanh_cell(last, t0, t0 + 2)
+        forget_times_cell(last, 0, 2)
+        input_times_candidate(last, 0, 2)
+        output_times_tanh(prev, 2, 4)
+        store(h_dram, h_new, prev, 0, N_TILES)
+        sum_to_cell(last, 0, 2)
+        store(c_dram, c_new, last, 0, 2)
+        tanh_cell(last, 0, 2)
+        forget_times_cell(last, 2, 4)
+        input_times_candidate(last, 2, 4)
+        output_times_tanh(last, 0, 2)
+        store(h_dram, h_new, last, 0, 2)
+        sum_to_cell(last, 2, 4)
+        store(c_dram, c_new, last, 2, 4)
+        tanh_cell(last, 2, 4)
         output_times_tanh(last, 2, 4)
         store(h_dram, h_new, last, 2, 4)

from contextlib import ExitStack

import concourse.mybir as mybir
from concourse.masks import make_identity

F32 = mybir.dt.float32
BF16 = mybir.dt.bfloat16
U32 = mybir.dt.uint32
U8 = mybir.dt.uint8
FP8X4 = mybir.dt.float8_e4m3fn_x4
ACT = mybir.ActivationFunctionType
ALU = mybir.AluOpType

BATCH = 512
HIDDEN = 1024
K_TOTAL = 2048
FLOPS = 2 * BATCH * K_TOTAL * 4 * HIDDEN

P = 128
N_TILES = BATCH // P
N_BLOCKS = HIDDEN // P
N_CHUNKS = 4
N_GATES = 4
GATE_COLS = N_GATES * P
CHUNK_WORDS = 256
ACTS = -1
RAW_BLOCKS = 5


def tile_structuredlstmcell_kernel(
    tc, p_in, hidden, cell, ext_input,
    W_pi, b_pi, W_pf, b_pf, W_pg, b_pg, W_po, b_po,
    W_hi, W_hf, W_hg, W_ho,
    W_xi, W_xf, W_xg, W_xo,
    out_0, out_1,
):
    nc = tc.nc
    weights = [
        [W_pi, W_pf, W_po, W_pg],
        [W_xi, W_xf, W_xo, W_xg],
        [W_hi, W_hf, W_ho, W_hg],
    ]
    biases = [b_pi, b_pf, b_po, b_pg]
    activations = [p_in, ext_input, hidden]
    k_of = [512, 512, 1024]
    col_i, col_f, col_o, col_g = [slice(g * P, (g + 1) * P) for g in range(N_GATES)]

    with ExitStack() as ctx:
        ctx.enter_context(tc.manual_schedule())
        const = ctx.enter_context(tc.tile_pool(name="const", bufs=1))
        raw_pool = ctx.enter_context(tc.tile_pool(name="raw", bufs=RAW_BLOCKS))
        grouped_pool = ctx.enter_context(tc.tile_pool(name="grouped", bufs=6))
        code_pool = ctx.enter_context(tc.tile_pool(name="codes", bufs=10))
        gate_pool = ctx.enter_context(tc.tile_pool(name="gates", bufs=4))
        out_pool = ctx.enter_context(tc.tile_pool(name="outs", bufs=3))
        psum = ctx.enter_context(tc.psum_pool(name="psum", bufs=1))

        ident_f32 = const.tile([P, P], F32, name="ident_f32")
        make_identity(nc, ident_f32[:])
        bias_rows = const.tile([P, GATE_COLS], BF16, name="bias_rows")
        nc.vector.memset(bias_rows[:], 0.0)
        warm = const.tile([P, 1], F32, name="warm")
        nc.vector.memset(warm[:], 0.0)
        for g in range(N_GATES):
            nc.scalar.dma_start(
                out=bias_rows[2 * g:2 * g + 2, :], in_=biases[g].rearrange("(r n) -> r n", r=2)
            )
        nc.scalar.activation(out=warm[:], in_=warm[:], func=ACT.Sigmoid)
        ident_bf16 = const.tile([P, P], BF16, name="ident_bf16")
        nc.vector.tensor_copy(out=ident_bf16[:], in_=ident_f32[:])
        bias_all = const.tile([P, N_GATES, HIDDEN], BF16, name="bias_all")
        cell_sb = const.tile([P, N_TILES, HIDDEN], BF16, name="cell_sb")
        act_codes = const.tile([P, N_CHUNKS, BATCH], U32, name="act_codes", align_bytes=64)
        act_scales = const.tile([P, N_CHUNKS, BATCH], U8, name="act_scales", align_bytes=64)

        raw = {}

        def load_activation(s):
            raw[(ACTS, s)] = const.tile([P, N_TILES * k_of[s]], BF16, name="raw_act%d" % s)
            view = activations[s].rearrange("(p t) k -> p (t k)", t=N_TILES)
            half_cols = 2 * k_of[s]
            for part in range(2):
                cols = slice(part * half_cols, (part + 1) * half_cols)
                nc.sync.dma_start(out=raw[(ACTS, s)][:, cols], in_=view[:, cols])

        def load_weights(j, s):
            k = k_of[s]
            raw[(j, s)] = raw_pool.tile([P, N_GATES * k], BF16, name="raw_w%d" % s, tag="raw_w%d" % s)
            for g in range(N_GATES):
                nc.sync.dma_start(out=raw[(j, s)][:, g * k:(g + 1) * k], in_=weights[s][g][j * P:(j + 1) * P, :])

        def load_block(j):
            for s in range(3):
                load_weights(j, s)

        for s in range(3):
            load_activation(s)
            load_weights(0, s)
        load_block(1)
        nc.sync.dma_start(
            out=cell_sb[:].rearrange("p t h -> p (t h)"), in_=cell.rearrange("(p t) h -> p (t h)", t=N_TILES)
        )
        for j in range(2, RAW_BLOCKS):
            load_block(j)

        free_banks = list(range(8))

        def take_bank(shape):
            b = free_banks.pop(0)
            return b, psum.tile(shape, F32, name="bank%d" % b, tag="bank%d" % b)

        grouped = {}
        w_codes = {}
        acc = {}
        gates = {}
        c_new = {}
        h_new = {}

        def transpose_chunk(j, c, engines):
            s = min(c, 2)
            first_word = CHUNK_WORDS * (c - 2) if c > 2 else 0
            words = raw[(j, s)][:].bitcast(F32)
            out_tile = grouped_pool.tile([P, 4 * GATE_COLS], BF16, name="grouped", tag="grouped", align_bytes=64)
            grouped[(j, c)] = out_tile
            out_words = out_tile[:].bitcast(F32)
            banks = []
            for half in range(2):
                b, bank = take_bank([P, 2, 2 * P])
                for rg in range(2):
                    for u in range(2):
                        col = (2 * half + rg) * (k_of[s] // 2) + first_word + P * u
                        nc.tensor.transpose(bank[:, u, rg * P:(rg + 1) * P], words[:, col:col + P], ident_f32[:])
                banks.append((b, bank))
            for half in range(2):
                b, bank = banks[half]
                dst = out_words[:, half * GATE_COLS:(half + 1) * GATE_COLS].rearrange("p (n u) -> p n u", u=2)
                src = bank[:].rearrange("p u n -> p n u")
                if engines[half] == "s":
                    nc.scalar.copy(out=dst, in_=src)
                else:
                    nc.vector.tensor_copy(out=dst, in_=src)
                free_banks.append(b)

        def quantise(j, c):
            if j == ACTS:
                codes, scales = act_codes[:, c, :], act_scales[:, c, :]
            else:
                codes_tile = code_pool.tile([P, GATE_COLS], U32, name="w_codes", tag="w_codes", align_bytes=64)
                scales_tile = code_pool.tile([P, GATE_COLS], U8, name="w_scales", tag="w_scales", align_bytes=64)
                w_codes[(j, c)] = (codes_tile, scales_tile)
                codes, scales = codes_tile[:], scales_tile[:]
            nc.vector.quantize_mx(out=codes.bitcast(FP8X4), scales=scales, in_=grouped[(j, c)][:])

        def mx_pass(j, t, c):
            if c == 0:
                acc[(j, t)] = take_bank([P, GATE_COLS])
            codes_tile, scales_tile = w_codes[(j, c)]
            rows = slice(t * P, (t + 1) * P)
            nc.tensor.matmul_mx(
                out=acc[(j, t)][1][:],
                lhsT=act_codes[:, c, rows].bitcast(FP8X4),
                lhsT_scale=act_scales[:, c, rows],
                rhs=codes_tile[:].bitcast(FP8X4),
                rhs_scale=scales_tile[:],
                start=(c == 0),
                stop=(c == N_CHUNKS - 1),
            )

        def spread_bias(first_row):
            for r in range(first_row, first_row + 4):
                b, bank = take_bank([P, GATE_COLS])
                nc.tensor.matmul(
                    out=bank[:], lhsT=ident_bf16[:, r:r + 1].to_broadcast([P, P]), rhs=bias_rows[:], start=True, stop=True
                )
                dst = bias_all[:, r // 2, (r % 2) * GATE_COLS:(r % 2 + 1) * GATE_COLS]
                if r % 2 == 0:
                    nc.scalar.copy(out=dst, in_=bank[:])
                else:
                    nc.vector.tensor_copy(out=dst, in_=bank[:])
                free_banks.append(b)

        def add_bias(j, t):
            if t == 0:
                gates[j] = gate_pool.tile([P, N_TILES, GATE_COLS], F32, name="gates", tag="gates")
            b, bank = acc[(j, t)]
            nc.vector.tensor_tensor(
                out=gates[j][:, t, :].rearrange("p (g n) -> p g n", g=N_GATES),
                in0=bank[:].rearrange("p (g n) -> p g n", g=N_GATES),
                in1=bias_all[:, :, j * P:(j + 1) * P],
                op=ALU.add,
            )
            free_banks.append(b)

        def passes_and_bias(j, t):
            for c in range(N_CHUNKS):
                mx_pass(j, t, c)
            add_bias(j, t)

        def sigmoids(j, t0, t1):
            v = gates[j][:, t0:t1, 0:3 * P]
            nc.scalar.activation(out=v, in_=v, func=ACT.Sigmoid)

        def tanh_candidate(j, t0, t1):
            v = gates[j][:, t0:t1, col_g]
            nc.scalar.activation(out=v, in_=v, func=ACT.Tanh)

        def forget_times_cell(j, t0, t1):
            v = gates[j][:, t0:t1, col_f]
            nc.vector.tensor_tensor(out=v, in0=v, in1=cell_sb[:, t0:t1, j * P:(j + 1) * P], op=ALU.mult)

        def input_times_candidate(j, t0, t1):
            v = gates[j][:, t0:t1, col_i]
            nc.vector.tensor_tensor(out=v, in0=v, in1=gates[j][:, t0:t1, col_g], op=ALU.mult)

        def sum_to_cell(j, t0, t1):
            if j not in c_new:
                c_new[j] = out_pool.tile([P, N_TILES, P], F32, name="c_new", tag="c_new")
            nc.vector.tensor_tensor(
                out=c_new[j][:, t0:t1, :], in0=gates[j][:, t0:t1, col_f], in1=gates[j][:, t0:t1, col_i], op=ALU.add
            )

        def tanh_cell(j, t0, t1):
            nc.scalar.activation(out=gates[j][:, t0:t1, col_g], in_=c_new[j][:, t0:t1, :], func=ACT.Tanh)

        def output_times_tanh(j, t0, t1):
            if j not in h_new:
                h_new[j] = out_pool.tile([P, N_TILES, P], F32, name="h_new", tag="h_new")
            nc.vector.tensor_tensor(
                out=h_new[j][:, t0:t1, :], in0=gates[j][:, t0:t1, col_o], in1=gates[j][:, t0:t1, col_g], op=ALU.mult
            )

        h_dram = out_0.rearrange("(p t) h -> p t h", t=N_TILES)
        c_dram = out_1.rearrange("(p t) h -> p t h", t=N_TILES)

        def store(dram, tiles, j, t0, t1):
            nc.sync.dma_start(out=dram[:, t0:t1, j * P:(j + 1) * P], in_=tiles[j][:, t0:t1, :])

        transpose_chunk(ACTS, 0, "sv")
        spread_bias(0)
        transpose_chunk(0, 0, "sv")
        quantise(ACTS, 0)
        transpose_chunk(ACTS, 1, "sv")
        quantise(0, 0)
        spread_bias(4)
        transpose_chunk(0, 1, "sv")
        quantise(ACTS, 1)
        transpose_chunk(ACTS, 2, "ss")
        quantise(0, 1)
        transpose_chunk(ACTS, 3, "ss")
        for c in (0, 1):
            for t in range(N_TILES):
                mx_pass(0, t, c)
        quantise(ACTS, 2)
        quantise(ACTS, 3)
        transpose_chunk(0, 2, "ss")
        transpose_chunk(0, 3, "ss")
        load_block(RAW_BLOCKS)
        quantise(0, 2)
        quantise(0, 3)
        transpose_chunk(1, 0, "ss")
        transpose_chunk(1, 1, "ss")
        for c in (2, 3):
            for t in range(N_TILES):
                mx_pass(0, t, c)
        quantise(1, 0)
        quantise(1, 1)
        for t in range(N_TILES):
            add_bias(0, t)
        transpose_chunk(1, 2, "ss")
        transpose_chunk(1, 3, "ss")
        load_block(RAW_BLOCKS + 1)
        quantise(1, 2)
        quantise(1, 3)

        for j in range(1, N_BLOCKS - 1):
            transpose_chunk(j + 1, 0, "ss")
            transpose_chunk(j + 1, 1, "ss")
            quantise(j + 1, 0)
            quantise(j + 1, 1)
            sigmoids(j - 1, 0, N_TILES)
            tanh_candidate(j - 1, 0, N_TILES)
            passes_and_bias(j, 0)
            passes_and_bias(j, 1)
            forget_times_cell(j - 1, 0, N_TILES)
            input_times_candidate(j - 1, 0, N_TILES)
            sum_to_cell(j - 1, 0, N_TILES)
            store(c_dram, c_new, j - 1, 0, N_TILES)
            transpose_chunk(j + 1, 2, "ss")
            transpose_chunk(j + 1, 3, "ss")
            if j + 1 + RAW_BLOCKS < N_BLOCKS:
                load_block(j + 1 + RAW_BLOCKS)
            tanh_cell(j - 1, 0, N_TILES)
            quantise(j + 1, 2)
            quantise(j + 1, 3)
            passes_and_bias(j, 2)
            output_times_tanh(j - 1, 0, N_TILES)
            store(h_dram, h_new, j - 1, 0, N_TILES)
            passes_and_bias(j, 3)

        last = N_BLOCKS - 1
        prev = last - 1
        sigmoids(prev, 0, 2)
        tanh_candidate(prev, 0, 2)
        sigmoids(prev, 2, 4)
        tanh_candidate(prev, 2, 4)
        forget_times_cell(prev, 0, 2)
        passes_and_bias(last, 0)
        input_times_candidate(prev, 0, 2)
        passes_and_bias(last, 1)
        sum_to_cell(prev, 0, 2)
        forget_times_cell(prev, 2, 4)
        sigmoids(last, 0, 2)
        tanh_cell(prev, 0, 2)
        tanh_candidate(last, 0, 2)
        passes_and_bias(last, 2)
        output_times_tanh(prev, 0, 2)
        passes_and_bias(last, 3)
        input_times_candidate(prev, 2, 4)
        sum_to_cell(prev, 2, 4)
        store(c_dram, c_new, prev, 0, N_TILES)
        sigmoids(last, 2, 4)
        tanh_cell(prev, 2, 4)
        tanh_candidate(last, 2, 4)
        forget_times_cell(last, 0, 2)
        input_times_candidate(last, 0, 2)
        output_times_tanh(prev, 2, 4)
        store(h_dram, h_new, prev, 0, N_TILES)
        sum_to_cell(last, 0, 2)
        store(c_dram, c_new, last, 0, 2)
        tanh_cell(last, 0, 2)
        forget_times_cell(last, 2, 4)
        input_times_candidate(last, 2, 4)
        output_times_tanh(last, 0, 2)
        store(h_dram, h_new, last, 0, 2)
        sum_to_cell(last, 2, 4)
        store(c_dram, c_new, last, 2, 4)
        tanh_cell(last, 2, 4)
        output_times_tanh(last, 2, 4)
        store(h_dram, h_new, last, 2, 4)
